import numpy as np
import ml_dtypes


def mxq(x, axis, fmt="e4m3"):
    dtype, down = {"e4m3": (ml_dtypes.float8_e4m3fn, 7), "e5m2": (ml_dtypes.float8_e5m2, 14)}[fmt]
    v = np.moveaxis(np.asarray(x, np.float32).astype(ml_dtypes.bfloat16).astype(np.float64), axis, -1)
    blocks = v.reshape(v.shape[:-1] + (-1, 32))
    amax = np.abs(blocks).max(-1, keepdims=True)
    byte = np.maximum(np.where(amax > 0, np.frexp(amax)[1] - 1 + 127, 0) - down, 1)
    scale = np.exp2(byte - 127.0)
    codes = (blocks / scale).astype(np.float32).astype(dtype).astype(np.float64)
    return np.moveaxis((codes * scale).reshape(v.shape), -1, axis)


WIDE = False


def mx_kscale(k):
    if not WIDE:
        return np.ones(k)
    levels = np.array([10, -10, 5, -5, 0])
    a = np.random.permutation(np.resize(levels, k // 512 * 4)).reshape(k // 512, 4)
    idx = np.arange(k)
    return np.exp2(a[idx // 512, idx % 128 // 32])


BF16 = ml_dtypes.bfloat16


def bf(x):
    return np.asarray(x, np.float32).astype(BF16)


def f64(x):
    return np.asarray(x).astype(np.float64)


B, P, D = 256, 2, 512
IN = P * D


def sigmoid(v):
    return 1.0 / (1.0 + np.exp(-v))


def setup_inputs():
    s = mx_kscale(D)
    sf = np.tile(s, P)
    return {"x": bf(np.random.standard_normal((B, IN)) * sf),
            "weights": bf(np.random.standard_normal((P, D, D)) / np.sqrt(D) / s[None, :, None] * s[None, None, :]),
            "bias": bf(np.random.standard_normal(IN) * 0.3 * sf),
            "gain": bf(1.3 + 0.1 * np.random.standard_normal(1)),
            "norm_bias": bf((0.3 + 0.05 * np.random.standard_normal(1)) * s.min()),
            "gamma": bf(0.5 + 0.3 * np.random.standard_normal(IN)),
            "beta": bf(np.random.standard_normal(IN) / sf)}


def reference(x, weights, bias, gain, norm_bias, gamma, beta):
    x, gamma = f64(x), f64(gamma)
    x_norm = x * f64(gain) + f64(norm_bias)
    xp = x_norm.reshape(B, P, D)
    yp = mxq(xp, 2, "e4m3").transpose(1, 0, 2) @ mxq(f64(weights), 1, "e4m3")
    y = yp.transpose(1, 0, 2).reshape(B, IN) + f64(bias)
    mult = gamma + sigmoid(f64(beta) * y) * (1.0 - gamma)
    o = mult * y
    return o + x

@@ -1,0 +1,185 @@
+from contextlib import ExitStack
+
+import concourse.masks as masks
+import concourse.mybir as mybir
+
+F32 = mybir.dt.float32
+BF16 = mybir.dt.bfloat16
+U32 = mybir.dt.uint32
+U8 = mybir.dt.uint8
+FP8X4 = mybir.dt.float8_e4m3fn_x4
+ACT = mybir.ActivationFunctionType
+ALU = mybir.AluOpType
+
+P = 128
+PACK = 4
+BATCH = 256
+PARTS = 2
+D = 512
+ROW_TILES = BATCH // P
+COL_TILES = D // P
+HALVES = 2
+PAIR = 2
+
+FLOPS = 2 * BATCH * PARTS * D * D
+
+
+def tile_better_transformer_s_kernel(tc, x, weights, bias, gain, norm_bias, gamma, beta, out):
+    nc = tc.nc
+    with ExitStack() as ctx:
+        consts = ctx.enter_context(tc.tile_pool(name="consts", bufs=1))
+        parts = ctx.enter_context(tc.tile_pool(name="parts", bufs=1))
+        work = ctx.enter_context(tc.tile_pool(name="work", bufs=4))
+        psum_t = ctx.enter_context(tc.psum_pool(name="psum_t", bufs=3))
+        psum_y = ctx.enter_context(tc.psum_pool(name="psum_y", bufs=5))
+
+        x_raw = []
+        w_raw = []
+        for p in range(PARTS):
+            x_part = parts.tile([P, ROW_TILES, D], BF16, name="x_raw%d" % p)
+            nc.sync.dma_start(
+                out=x_part[:], in_=x[:, p * D : (p + 1) * D].rearrange("(i b) k -> b i k", b=P)
+            )
+            x_raw.append(x_part)
+            w_part = parts.tile([P, PACK, D], BF16, name="w_raw%d" % p)
+            nc.sync.dma_start(
+                out=w_part[:].rearrange("q (u e) c -> q u (e c)", u=HALVES),
+                in_=weights[p].rearrange("(u q e) c -> q u (e c)", u=HALVES, e=PAIR),
+            )
+            w_raw.append(w_part)
+
+        gain_bf = consts.tile([P, 1], BF16)
+        shift_bf = consts.tile([P, 1], BF16)
+        with nc.allow_non_contiguous_dma(reason="one bfloat16 number to each partition"):
+            nc.scalar.dma_start(out=gain_bf[:], in_=gain.partition_broadcast(P))
+            nc.scalar.dma_start(out=shift_bf[:], in_=norm_bias.partition_broadcast(P))
+        n_tiles = PARTS * COL_TILES
+        vec_rows = consts.tile([P, P], BF16)
+        nc.vector.memset(vec_rows[:], 0.0)
+        for r, vec in enumerate((bias, gamma, beta)):
+            nc.scalar.dma_start(
+                out=vec_rows[r * n_tiles : (r + 1) * n_tiles, :], in_=vec.rearrange("(j c) -> j c", c=P)
+            )
+
+        warm_in = consts.tile([P, 1], F32)
+        warm_out = consts.tile([P, 1], F32)
+        nc.vector.memset(warm_in[:], 0.0)
+        nc.scalar.activation(out=warm_out[:], in_=warm_in[:], func=ACT.Sigmoid)
+
+        ident_f32 = consts.tile([P, P], F32)
+        masks.make_identity(nc, ident_f32[:])
+        ident_bf = consts.tile([P, P], BF16)
+        masks.make_identity(nc, ident_bf[:])
+
+        gain_f32 = consts.tile([P, 1], F32)
+        shift_f32 = consts.tile([P, 1], F32)
+        nc.vector.tensor_copy(out=gain_f32[:], in_=gain_bf[:])
+        nc.vector.tensor_copy(out=shift_f32[:], in_=shift_bf[:])
+
+        x_codes = []
+        x_scales = []
+        x_grouped = []
+        for p in range(PARTS):
+            x_words = x_raw[p][:].rearrange("b i k -> b (i k)").bitcast(F32)
+            words_per_row = D // PAIR
+            x_t = psum_t.tile([P, HALVES, BATCH], F32, tag="t", name="x_t%d" % p)
+            for i in range(ROW_TILES):
+                for u in range(HALVES):
+                    first = i * words_per_row + u * P
+                    nc.tensor.transpose(
+                        x_t[:, u, i * P : (i + 1) * P], x_words[:, first : first + P], ident_f32[:]
+                    )
+            grouped = parts.tile([P, BATCH, PACK], BF16, name="x_grouped%d" % p, align_bytes=64)
+            nc.scalar.activation(
+                out=grouped[:].rearrange("q b (u e) -> q b u e", u=HALVES),
+                in_=x_t[:].rearrange("q u b -> q (u b)").bitcast(BF16).rearrange(
+                    "q (u b e) -> q b u e", u=HALVES, e=PAIR
+                ),
+                func=ACT.Identity,
+                bias=shift_f32[:],
+                scale=gain_f32[:],
+            )
+            x_grouped.append(grouped)
+
+        vec_t = psum_t.tile([P, P], BF16, tag="t")
+        nc.tensor.transpose(vec_t[:], vec_rows[:], ident_bf[:])
+        vec_cols = consts.tile([P, 3 * n_tiles], F32)
+        nc.vector.tensor_copy(out=vec_cols[:], in_=vec_t[:, 0 : 3 * n_tiles])
+        bias_col = vec_cols[:, 0:n_tiles]
+        gamma_col = vec_cols[:, n_tiles : 2 * n_tiles]
+        beta_col = vec_cols[:, 2 * n_tiles : 3 * n_tiles]
+        beta_bias_col = consts.tile([P, n_tiles], F32)
+        nc.vector.tensor_mul(out=beta_bias_col[:], in0=beta_col, in1=bias_col)
+        rest_col = consts.tile([P, n_tiles], F32)
+        nc.vector.tensor_scalar(
+            out=rest_col[:], in0=gamma_col, scalar1=-1.0, scalar2=1.0, op0=ALU.mult, op1=ALU.add
+        )
+
+        w_codes = []
+        w_scales = []
+        for p in range(PARTS):
+            w_grouped = parts.tile([P, D, PACK], BF16, name="w_grouped%d" % p, align_bytes=64)
+            nc.vector.tensor_copy(
+                out=w_grouped[:].rearrange("q (c r) t -> q c t r", r=4),
+                in_=w_raw[p][:].rearrange("q t (c r) -> q c t r", r=4),
+            )
+            xc = parts.tile([P, BATCH], U32, name="x_codes%d" % p, align_bytes=64)
+            xs = parts.tile([P, BATCH], U8, name="x_scales%d" % p, align_bytes=64)
+            nc.vector.quantize_mx(
+                out=xc[:].bitcast(FP8X4), scales=xs[:], in_=x_grouped[p][:].rearrange("q b t -> q (b t)")
+            )
+            wc = parts.tile([P, D], U32, name="w_codes%d" % p, align_bytes=64)
+            ws = parts.tile([P, D], U8, name="w_scales%d" % p, align_bytes=64)
+            nc.vector.quantize_mx(
+                out=wc[:].bitcast(FP8X4), scales=ws[:], in_=w_grouped[:].rearrange("q c t -> q (c t)")
+            )
+            x_codes.append(xc)
+            x_scales.append(xs)
+            w_codes.append(wc)
+            w_scales.append(ws)
+
+        y_t = []
+        for p in range(PARTS):
+            for jj in range(COL_TILES):
+                cols = slice(jj * P, (jj + 1) * P)
+                acc = psum_y.tile([P, BATCH], F32, tag="y", name="y_t%d" % (p * COL_TILES + jj))
+                nc.tensor.matmul_mx(
+                    out=acc[:],
+                    lhsT=w_codes[p][:, cols].bitcast(FP8X4),
+                    lhsT_scale=w_scales[p][:, cols],
+                    rhs=x_codes[p][:].bitcast(FP8X4),
+                    rhs_scale=x_scales[p][:],
+                    start=True,
+                    stop=True,
+                )
+                y_t.append(acc)
+
+        for p in range(PARTS):
+            back = []
+            for i in range(ROW_TILES):
+                back_tile = psum_t.tile([P, D], F32, tag="t", name="back%d_%d" % (p, i))
+                back.append(back_tile)
+            for jj in range(COL_TILES):
+                j = p * COL_TILES + jj
+                col = slice(j, j + 1)
+                sig = work.tile([P, BATCH], F32, tag="sig")
+                nc.scalar.activation(
+                    out=sig[:], in_=y_t[j][:], func=ACT.Sigmoid, bias=beta_bias_col[:, col], scale=beta_col[:, col]
+                )
+                mult = work.tile([P, BATCH], F32, tag="mult")
+                nc.vector.tensor_scalar(
+                    out=mult[:], in0=sig[:], scalar1=rest_col[:, col], scalar2=gamma_col[:, col],
+                    op0=ALU.mult, op1=ALU.add,
+                )
+                act_t = work.tile([P, BATCH], F32, tag="act_t")
+                nc.vector.scalar_tensor_tensor(
+                    out=act_t[:], in0=y_t[j][:], scalar=bias_col[:, col], in1=mult[:], op0=ALU.add, op1=ALU.mult
+                )
+                for i in range(ROW_TILES):
+                    nc.tensor.transpose(
+                        back[i][:, jj * P : (jj + 1) * P], act_t[:, i * P : (i + 1) * P], ident_f32[:]
+                    )
+            for i in range(ROW_TILES):
+                result = work.tile([P, D], F32, tag="result")
+                nc.vector.tensor_tensor(out=result[:], in0=back[i][:], in1=x_raw[p][:, i, :], op=ALU.add)
+                nc.sync.dma_start(out=out[i * P : (i + 1) * P, p * D : (p + 1) * D], in_=result[:])

@@ -26,72 +26,59 @@ FLOPS = 2 * BATCH * PARTS * D * D
 
 def tile_better_transformer_s_kernel(tc, x, weights, bias, gain, norm_bias, gamma, beta, out):
     nc = tc.nc
+    n_tiles = PARTS * COL_TILES
     with ExitStack() as ctx:
         consts = ctx.enter_context(tc.tile_pool(name="consts", bufs=1))
         parts = ctx.enter_context(tc.tile_pool(name="parts", bufs=1))
         work = ctx.enter_context(tc.tile_pool(name="work", bufs=4))
-        psum_t = ctx.enter_context(tc.psum_pool(name="psum_t", bufs=3))
-        psum_y = ctx.enter_context(tc.psum_pool(name="psum_y", bufs=5))
+        psum = ctx.enter_context(tc.psum_pool(name="psum", bufs=8))
+        ctx.enter_context(tc.manual_schedule())
 
-        x_raw = []
-        w_raw = []
-        for p in range(PARTS):
-            x_part = parts.tile([P, ROW_TILES, D], BF16, name="x_raw%d" % p)
-            nc.sync.dma_start(
-                out=x_part[:], in_=x[:, p * D : (p + 1) * D].rearrange("(i b) k -> b i k", b=P)
-            )
-            x_raw.append(x_part)
-            w_part = parts.tile([P, PACK, D], BF16, name="w_raw%d" % p)
-            nc.sync.dma_start(
-                out=w_part[:].rearrange("q (u e) c -> q u (e c)", u=HALVES),
-                in_=weights[p].rearrange("(u q e) c -> q u (e c)", u=HALVES, e=PAIR),
-            )
-            w_raw.append(w_part)
-
+        x_raw = [parts.tile([P, ROW_TILES, D], BF16, name="x_raw%d" % p) for p in range(PARTS)]
+        w_raw = [parts.tile([P, PACK, D], BF16, name="w_raw%d" % p) for p in range(PARTS)]
+        x_grouped = [parts.tile([P, BATCH, PACK], BF16, name="x_grouped%d" % p, align_bytes=64) for p in range(PARTS)]
+        w_grouped = [parts.tile([P, D, PACK], BF16, name="w_grouped%d" % p, align_bytes=64) for p in range(PARTS)]
+        x_codes = [parts.tile([P, BATCH], U32, name="x_codes%d" % p, align_bytes=64) for p in range(PARTS)]
+        x_scales = [parts.tile([P, BATCH], U8, name="x_scales%d" % p, align_bytes=64) for p in range(PARTS)]
+        w_codes = [parts.tile([P, D], U32, name="w_codes%d" % p, align_bytes=64) for p in range(PARTS)]
+        w_scales = [parts.tile([P, D], U8, name="w_scales%d" % p, align_bytes=64) for p in range(PARTS)]
         gain_bf = consts.tile([P, 1], BF16)
         shift_bf = consts.tile([P, 1], BF16)
-        with nc.allow_non_contiguous_dma(reason="one bfloat16 number to each partition"):
-            nc.scalar.dma_start(out=gain_bf[:], in_=gain.partition_broadcast(P))
-            nc.scalar.dma_start(out=shift_bf[:], in_=norm_bias.partition_broadcast(P))
-        n_tiles = PARTS * COL_TILES
-        vec_rows = consts.tile([P, P], BF16)
-        nc.vector.memset(vec_rows[:], 0.0)
-        for r, vec in enumerate((bias, gamma, beta)):
-            nc.scalar.dma_start(
-                out=vec_rows[r * n_tiles : (r + 1) * n_tiles, :], in_=vec.rearrange("(j c) -> j c", c=P)
-            )
-
-        warm_in = consts.tile([P, 1], F32)
-        warm_out = consts.tile([P, 1], F32)
-        nc.vector.memset(warm_in[:], 0.0)
-        nc.scalar.activation(out=warm_out[:], in_=warm_in[:], func=ACT.Sigmoid)
-
-        ident_f32 = consts.tile([P, P], F32)
-        masks.make_identity(nc, ident_f32[:])
-        ident_bf = consts.tile([P, P], BF16)
-        masks.make_identity(nc, ident_bf[:])
-
         gain_f32 = consts.tile([P, 1], F32)
         shift_f32 = consts.tile([P, 1], F32)
-        nc.vector.tensor_copy(out=gain_f32[:], in_=gain_bf[:])
-        nc.vector.tensor_copy(out=shift_f32[:], in_=shift_bf[:])
+        vec_rows = consts.tile([P, P], BF16)
+        vec_cols = consts.tile([P, 3 * n_tiles], F32)
+        bias_col = vec_cols[:, 0:n_tiles]
+        gamma_col = vec_cols[:, n_tiles : 2 * n_tiles]
+        beta_col = vec_cols[:, 2 * n_tiles : 3 * n_tiles]
+        beta_bias_col = consts.tile([P, n_tiles], F32)
+        rest_col = consts.tile([P, n_tiles], F32)
+        warm_in = consts.tile([P, 1], F32)
+        warm_out = consts.tile([P, 1], F32)
+        ident_f32 = consts.tile([P, P], F32)
+        ident_bf = consts.tile([P, P], BF16)
 
-        x_codes = []
-        x_scales = []
-        x_grouped = []
-        for p in range(PARTS):
+        def load_part(p):
+            nc.sync.dma_start(
+                out=w_raw[p][:].rearrange("q (u e) c -> q u (e c)", u=HALVES),
+                in_=weights[p].rearrange("(u q e) c -> q u (e c)", u=HALVES, e=PAIR),
+            )
+            nc.sync.dma_start(
+                out=x_raw[p][:], in_=x[:, p * D : (p + 1) * D].rearrange("(i b) k -> b i k", b=P)
+            )
+
+        def normalise_x(p):
             x_words = x_raw[p][:].rearrange("b i k -> b (i k)").bitcast(F32)
             words_per_row = D // PAIR
-            x_t = psum_t.tile([P, HALVES, BATCH], F32, tag="t", name="x_t%d" % p)
+            x_t = psum.tile([P, HALVES, BATCH], F32, tag="bank", name="x_t%d" % p)
             for i in range(ROW_TILES):
                 for u in range(HALVES):
                     first = i * words_per_row + u * P
                     nc.tensor.transpose(
                         x_t[:, u, i * P : (i + 1) * P], x_words[:, first : first + P], ident_f32[:]
                     )
-            grouped = parts.tile([P, BATCH, PACK], BF16, name="x_grouped%d" % p, align_bytes=64)
             nc.scalar.activation(
-                out=grouped[:].rearrange("q b (u e) -> q b u e", u=HALVES),
+                out=x_grouped[p][:].rearrange("q b (u e) -> q b u e", u=HALVES),
                 in_=x_t[:].rearrange("q u b -> q (u b)").bitcast(BF16).rearrange(
                     "q (u b e) -> q b u e", u=HALVES, e=PAIR
                 ),
@@ -99,50 +86,37 @@ def tile_better_transformer_s_kernel(tc, x, weights, bias, gain, norm_bias, gamm
                 bias=shift_f32[:],
                 scale=gain_f32[:],
             )
-            x_grouped.append(grouped)
 
-        vec_t = psum_t.tile([P, P], BF16, tag="t")
-        nc.tensor.transpose(vec_t[:], vec_rows[:], ident_bf[:])
-        vec_cols = consts.tile([P, 3 * n_tiles], F32)
-        nc.vector.tensor_copy(out=vec_cols[:], in_=vec_t[:, 0 : 3 * n_tiles])
-        bias_col = vec_cols[:, 0:n_tiles]
-        gamma_col = vec_cols[:, n_tiles : 2 * n_tiles]
-        beta_col = vec_cols[:, 2 * n_tiles : 3 * n_tiles]
-        beta_bias_col = consts.tile([P, n_tiles], F32)
-        nc.vector.tensor_mul(out=beta_bias_col[:], in0=beta_col, in1=bias_col)
-        rest_col = consts.tile([P, n_tiles], F32)
-        nc.vector.tensor_scalar(
-            out=rest_col[:], in0=gamma_col, scalar1=-1.0, scalar2=1.0, op0=ALU.mult, op1=ALU.add
-        )
+        def regroup_w(p):
+            for h in range(HALVES):
+                cols = slice(h * D // HALVES, (h + 1) * D // HALVES)
+                nc.vector.tensor_copy(
+                    out=w_grouped[p][:, cols, :].rearrange("q (c r) t -> q c t r", r=4),
+                    in_=w_raw[p][:, :, cols].rearrange("q t (c r) -> q c t r", r=4),
+                )
 
-        w_codes = []
-        w_scales = []
-        for p in range(PARTS):
-            w_grouped = parts.tile([P, D, PACK], BF16, name="w_grouped%d" % p, align_bytes=64)
-            nc.vector.tensor_copy(
-                out=w_grouped[:].rearrange("q (c r) t -> q c t r", r=4),
-                in_=w_raw[p][:].rearrange("q t (c r) -> q c t r", r=4),
-            )
-            xc = parts.tile([P, BATCH], U32, name="x_codes%d" % p, align_bytes=64)
-            xs = parts.tile([P, BATCH], U8, name="x_scales%d" % p, align_bytes=64)
+        def quantise_w(p):
+            for h in range(HALVES):
+                cols = slice(h * D // HALVES, (h + 1) * D // HALVES)
+                nc.vector.quantize_mx(
+                    out=w_codes[p][:, cols].bitcast(FP8X4),
+                    scales=w_scales[p][:, cols],
+                    in_=w_grouped[p][:, cols, :].rearrange("q c t -> q (c t)"),
+                )
+
+        def quantise_x(p):
             nc.vector.quantize_mx(
-                out=xc[:].bitcast(FP8X4), scales=xs[:], in_=x_grouped[p][:].rearrange("q b t -> q (b t)")
+                out=x_codes[p][:].bitcast(FP8X4),
+                scales=x_scales[p][:],
+                in_=x_grouped[p][:].rearrange("q b t -> q (b t)"),
             )
-            wc = parts.tile([P, D], U32, name="w_codes%d" % p, align_bytes=64)
-            ws = parts.tile([P, D], U8, name="w_scales%d" % p, align_bytes=64)
-            nc.vector.quantize_mx(
-                out=wc[:].bitcast(FP8X4), scales=ws[:], in_=w_grouped[:].rearrange("q c t -> q (c t)")
-            )
-            x_codes.append(xc)
-            x_scales.append(xs)
-            w_codes.append(wc)
-            w_scales.append(ws)
 
         y_t = []
-        for p in range(PARTS):
+
+        def multiply(p):
             for jj in range(COL_TILES):
                 cols = slice(jj * P, (jj + 1) * P)
-                acc = psum_y.tile([P, BATCH], F32, tag="y", name="y_t%d" % (p * COL_TILES + jj))
+                acc = psum.tile([P, BATCH], F32, tag="bank", name="y_t%d" % (p * COL_TILES + jj))
                 nc.tensor.matmul_mx(
                     out=acc[:],
                     lhsT=w_codes[p][:, cols].bitcast(FP8X4),
@@ -154,32 +128,81 @@ def tile_better_transformer_s_kernel(tc, x, weights, bias, gain, norm_bias, gamm
                 )
                 y_t.append(acc)
 
-        for p in range(PARTS):
-            back = []
+        back = {}
+
+        def activate(j):
+            p = j // COL_TILES
+            jj = j % COL_TILES
+            col = slice(j, j + 1)
+            sig = work.tile([P, BATCH], F32, tag="sig")
+            nc.scalar.activation(
+                out=sig[:], in_=y_t[j][:], func=ACT.Sigmoid, bias=beta_bias_col[:, col], scale=beta_col[:, col]
+            )
+            mult = work.tile([P, BATCH], F32, tag="mult")
+            nc.gpsimd.tensor_scalar(
+                out=mult[:], in0=sig[:], scalar1=rest_col[:, col], scalar2=gamma_col[:, col],
+                op0=ALU.mult, op1=ALU.add,
+            )
+            act_t = work.tile([P, BATCH], F32, tag="act_t")
+            nc.vector.scalar_tensor_tensor(
+                out=act_t[:], in0=y_t[j][:], scalar=bias_col[:, col], in1=mult[:], op0=ALU.add, op1=ALU.mult
+            )
             for i in range(ROW_TILES):
-                back_tile = psum_t.tile([P, D], F32, tag="t", name="back%d_%d" % (p, i))
-                back.append(back_tile)
-            for jj in range(COL_TILES):
-                j = p * COL_TILES + jj
-                col = slice(j, j + 1)
-                sig = work.tile([P, BATCH], F32, tag="sig")
-                nc.scalar.activation(
-                    out=sig[:], in_=y_t[j][:], func=ACT.Sigmoid, bias=beta_bias_col[:, col], scale=beta_col[:, col]
+                if jj == 0:
+                    back[(p, i)] = psum.tile([P, D], F32, tag="bank", name="back%d_%d" % (p, i))
+                nc.tensor.transpose(
+                    back[(p, i)][:, jj * P : (jj + 1) * P], act_t[:, i * P : (i + 1) * P], ident_f32[:]
                 )
-                mult = work.tile([P, BATCH], F32, tag="mult")
-                nc.vector.tensor_scalar(
-                    out=mult[:], in0=sig[:], scalar1=rest_col[:, col], scalar2=gamma_col[:, col],
-                    op0=ALU.mult, op1=ALU.add,
-                )
-                act_t = work.tile([P, BATCH], F32, tag="act_t")
-                nc.vector.scalar_tensor_tensor(
-                    out=act_t[:], in0=y_t[j][:], scalar=bias_col[:, col], in1=mult[:], op0=ALU.add, op1=ALU.mult
-                )
-                for i in range(ROW_TILES):
-                    nc.tensor.transpose(
-                        back[i][:, jj * P : (jj + 1) * P], act_t[:, i * P : (i + 1) * P], ident_f32[:]
-                    )
-            for i in range(ROW_TILES):
-                result = work.tile([P, D], F32, tag="result")
-                nc.vector.tensor_tensor(out=result[:], in0=back[i][:], in1=x_raw[p][:, i, :], op=ALU.add)
-                nc.sync.dma_start(out=out[i * P : (i + 1) * P, p * D : (p + 1) * D], in_=result[:])
+
+        def add_residual_and_store(p, i):
+            result = work.tile([P, D], F32, tag="result")
+            nc.vector.tensor_tensor(out=result[:], in0=back[(p, i)][:], in1=x_raw[p][:, i, :], op=ALU.add)
+            nc.sync.dma_start(out=out[i * P : (i + 1) * P, p * D : (p + 1) * D], in_=result[:])
+
+        with nc.allow_non_contiguous_dma(reason="one bfloat16 number to each partition"):
+            nc.scalar.dma_start(out=gain_bf[:], in_=gain.partition_broadcast(P))
+            nc.scalar.dma_start(out=shift_bf[:], in_=norm_bias.partition_broadcast(P))
+        load_part(0)
+        nc.vector.memset(vec_rows[:], 0.0)
+        for r, vec in enumerate((bias, gamma, beta)):
+            nc.scalar.dma_start(
+                out=vec_rows[r * n_tiles : (r + 1) * n_tiles, :], in_=vec.rearrange("(j c) -> j c", c=P)
+            )
+        load_part(1)
+
+        nc.vector.memset(warm_in[:], 0.0)
+        nc.scalar.activation(out=warm_out[:], in_=warm_in[:], func=ACT.Sigmoid)
+        masks.make_identity(nc, ident_f32[:])
+        masks.make_identity(nc, ident_bf[:])
+        nc.vector.tensor_copy(out=gain_f32[:], in_=gain_bf[:])
+        nc.vector.tensor_copy(out=shift_f32[:], in_=shift_bf[:])
+
+        regroup_w(0)
+        normalise_x(0)
+        quantise_w(0)
+
+        vec_t = psum.tile([P, P], BF16, tag="bank")
+        nc.tensor.transpose(vec_t[:], vec_rows[:], ident_bf[:])
+        nc.vector.tensor_copy(out=vec_cols[:], in_=vec_t[:, 0 : 3 * n_tiles])
+        nc.vector.tensor_mul(out=beta_bias_col[:], in0=beta_col, in1=bias_col)
+        nc.vector.tensor_scalar(
+            out=rest_col[:], in0=gamma_col, scalar1=-1.0, scalar2=1.0, op0=ALU.mult, op1=ALU.add
+        )
+
+        regroup_w(1)
+        normalise_x(1)
+        quantise_x(0)
+        multiply(0)
+        quantise_w(1)
+        quantise_x(1)
+        multiply(1)
+
+        outputs = [(p, i) for p in range(PARTS) for i in range(ROW_TILES)]
+        stored = 0
+        for j in range(n_tiles):
+            activate(j)
+            if j >= COL_TILES and j % ROW_TILES == ROW_TILES - 1:
+                add_residual_and_store(*outputs[stored])
+                stored += 1
+        for p, i in outputs[stored:]:
+            add_residual_and_store(p, i)

@@ -18,8 +18,10 @@ PARTS = 2
 D = 512
 ROW_TILES = BATCH // P
 COL_TILES = D // P
-HALVES = 2
 PAIR = 2
+WORDS = PACK // PAIR
+W_PIECES = 2
+JOINT = 2
 
 FLOPS = 2 * BATCH * PARTS * D * D
 
@@ -59,28 +61,23 @@ def tile_better_transformer_s_kernel(tc, x, weights, bias, gain, norm_bias, gamm
         ident_bf = consts.tile([P, P], BF16)
 
         def load_part(p):
-            nc.sync.dma_start(
-                out=w_raw[p][:].rearrange("q (u e) c -> q u (e c)", u=HALVES),
-                in_=weights[p].rearrange("(u q e) c -> q u (e c)", u=HALVES, e=PAIR),
-            )
+            nc.sync.dma_start(out=w_raw[p][:], in_=weights[p].rearrange("(q t) c -> q t c", t=PACK))
             nc.sync.dma_start(
                 out=x_raw[p][:], in_=x[:, p * D : (p + 1) * D].rearrange("(i b) k -> b i k", b=P)
             )
 
         def normalise_x(p):
-            x_words = x_raw[p][:].rearrange("b i k -> b (i k)").bitcast(F32)
-            words_per_row = D // PAIR
-            x_t = psum.tile([P, HALVES, BATCH], F32, tag="bank", name="x_t%d" % p)
+            x_words = x_raw[p][:].rearrange("b i k -> b (i k)").bitcast(F32).rearrange(
+                "b (i q u) -> b i u q", i=ROW_TILES, u=WORDS
+            )
+            x_t = psum.tile([P, WORDS, BATCH], F32, tag="bank", name="x_t%d" % p)
             for i in range(ROW_TILES):
-                for u in range(HALVES):
-                    first = i * words_per_row + u * P
-                    nc.tensor.transpose(
-                        x_t[:, u, i * P : (i + 1) * P], x_words[:, first : first + P], ident_f32[:]
-                    )
+                for u in range(WORDS):
+                    nc.tensor.transpose(x_t[:, u, i * P : (i + 1) * P], x_words[:, i, u, :], ident_f32[:])
             nc.scalar.activation(
-                out=x_grouped[p][:].rearrange("q b (u e) -> q b u e", u=HALVES),
+                out=x_grouped[p][:].rearrange("q b (u e) -> q b u e", u=WORDS),
                 in_=x_t[:].rearrange("q u b -> q (u b)").bitcast(BF16).rearrange(
-                    "q (u b e) -> q b u e", u=HALVES, e=PAIR
+                    "q (u b e) -> q b u e", u=WORDS, e=PAIR
                 ),
                 func=ACT.Identity,
                 bias=shift_f32[:],
@@ -88,16 +85,16 @@ def tile_better_transformer_s_kernel(tc, x, weights, bias, gain, norm_bias, gamm
             )
 
         def regroup_w(p):
-            for h in range(HALVES):
-                cols = slice(h * D // HALVES, (h + 1) * D // HALVES)
+            for h in range(W_PIECES):
+                cols = slice(h * D // W_PIECES, (h + 1) * D // W_PIECES)
                 nc.vector.tensor_copy(
                     out=w_grouped[p][:, cols, :].rearrange("q (c r) t -> q c t r", r=4),
                     in_=w_raw[p][:, :, cols].rearrange("q t (c r) -> q c t r", r=4),
                 )
 
         def quantise_w(p):
-            for h in range(HALVES):
-                cols = slice(h * D // HALVES, (h + 1) * D // HALVES)
+            for h in range(W_PIECES):
+                cols = slice(h * D // W_PIECES, (h + 1) * D // W_PIECES)
                 nc.vector.quantize_mx(
                     out=w_codes[p][:, cols].bitcast(FP8X4),
                     scales=w_scales[p][:, cols],
@@ -131,8 +128,6 @@ def tile_better_transformer_s_kernel(tc, x, weights, bias, gain, norm_bias, gamm
         back = {}
 
         def activate(j):
-            p = j // COL_TILES
-            jj = j % COL_TILES
             col = slice(j, j + 1)
             sig = work.tile([P, BATCH], F32, tag="sig")
             nc.scalar.activation(
@@ -147,17 +142,24 @@ def tile_better_transformer_s_kernel(tc, x, weights, bias, gain, norm_bias, gamm
             nc.vector.scalar_tensor_tensor(
                 out=act_t[:], in0=y_t[j][:], scalar=bias_col[:, col], in1=mult[:], op0=ALU.add, op1=ALU.mult
             )
+            g = j // JOINT
+            place = j % JOINT
+            if place == 0:
+                back[g] = psum.tile([P, ROW_TILES, JOINT * P], F32, tag="bank", name="back%d" % g)
             for i in range(ROW_TILES):
-                if jj == 0:
-                    back[(p, i)] = psum.tile([P, D], F32, tag="bank", name="back%d_%d" % (p, i))
                 nc.tensor.transpose(
-                    back[(p, i)][:, jj * P : (jj + 1) * P], act_t[:, i * P : (i + 1) * P], ident_f32[:]
+                    back[g][:, i, place * P : (place + 1) * P], act_t[:, i * P : (i + 1) * P], ident_f32[:]
                 )
 
-        def add_residual_and_store(p, i):
-            result = work.tile([P, D], F32, tag="result")
-            nc.vector.tensor_tensor(out=result[:], in0=back[(p, i)][:], in1=x_raw[p][:, i, :], op=ALU.add)
-            nc.sync.dma_start(out=out[i * P : (i + 1) * P, p * D : (p + 1) * D], in_=result[:])
+        def add_residual_and_store(g):
+            width = JOINT * P
+            p = g * width // D
+            in_part = slice(g * width - p * D, (g + 1) * width - p * D)
+            result = work.tile([P, ROW_TILES, width], F32, tag="result")
+            nc.vector.tensor_tensor(out=result[:], in0=back[g][:], in1=x_raw[p][:, :, in_part], op=ALU.add)
+            nc.sync.dma_start(
+                out=out[:, g * width : (g + 1) * width].rearrange("(i b) c -> b i c", b=P), in_=result[:]
+            )
 
         with nc.allow_non_contiguous_dma(reason="one bfloat16 number to each partition"):
             nc.scalar.dma_start(out=gain_bf[:], in_=gain.partition_broadcast(P))
@@ -197,12 +199,8 @@ def tile_better_transformer_s_kernel(tc, x, weights, bias, gain, norm_bias, gamm
         quantise_x(1)
         multiply(1)
 
-        outputs = [(p, i) for p in range(PARTS) for i in range(ROW_TILES)]
-        stored = 0
         for j in range(n_tiles):
             activate(j)
-            if j >= COL_TILES and j % ROW_TILES == ROW_TILES - 1:
-                add_residual_and_store(*outputs[stored])
-                stored += 1
-        for p, i in outputs[stored:]:
-            add_residual_and_store(p, i)
+            if j >= JOINT and j % JOINT == 0:
+                add_residual_and_store(j // JOINT - 1)
+        add_residual_and_store(n_tiles // JOINT - 1)

@@ -134,7 +134,8 @@ def tile_better_transformer_s_kernel(tc, x, weights, bias, gain, norm_bias, gamm
                 out=sig[:], in_=y_t[j][:], func=ACT.Sigmoid, bias=beta_bias_col[:, col], scale=beta_col[:, col]
             )
             mult = work.tile([P, BATCH], F32, tag="mult")
-            nc.gpsimd.tensor_scalar(
+            mult_engine = nc.vector if j < COL_TILES else nc.gpsimd
+            mult_engine.tensor_scalar(
                 out=mult[:], in0=sig[:], scalar1=rest_col[:, col], scalar2=gamma_col[:, col],
                 op0=ALU.mult, op1=ALU.add,
             )
@@ -201,6 +202,6 @@ def tile_better_transformer_s_kernel(tc, x, weights, bias, gain, norm_bias, gamm
 
         for j in range(n_tiles):
             activate(j)
-            if j >= JOINT and j % JOINT == 0:
+            if j % JOINT == JOINT - 1 and j >= 2 * JOINT - 1:
                 add_residual_and_store(j // JOINT - 1)
         add_residual_and_store(n_tiles // JOINT - 1)

@@ -22,6 +22,7 @@ PAIR = 2
 WORDS = PACK // PAIR
 W_PIECES = 2
 JOINT = 2
+S_COLS = 192
 
 FLOPS = 2 * BATCH * PARTS * D * D
 
@@ -66,17 +67,21 @@ def tile_better_transformer_s_kernel(tc, x, weights, bias, gain, norm_bias, gamm
                 out=x_raw[p][:], in_=x[:, p * D : (p + 1) * D].rearrange("(i b) k -> b i k", b=P)
             )
 
-        def normalise_x(p):
+        x_t = {}
+
+        def x_transposes(p):
             x_words = x_raw[p][:].rearrange("b i k -> b (i k)").bitcast(F32).rearrange(
                 "b (i q u) -> b i u q", i=ROW_TILES, u=WORDS
             )
-            x_t = psum.tile([P, WORDS, BATCH], F32, tag="bank", name="x_t%d" % p)
+            x_t[p] = psum.tile([P, WORDS, BATCH], F32, tag="bank", name="x_t%d" % p)
             for i in range(ROW_TILES):
                 for u in range(WORDS):
-                    nc.tensor.transpose(x_t[:, u, i * P : (i + 1) * P], x_words[:, i, u, :], ident_f32[:])
+                    nc.tensor.transpose(x_t[p][:, u, i * P : (i + 1) * P], x_words[:, i, u, :], ident_f32[:])
+
+        def normalise_x(p):
             nc.scalar.activation(
                 out=x_grouped[p][:].rearrange("q b (u e) -> q b u e", u=WORDS),
-                in_=x_t[:].rearrange("q u b -> q (u b)").bitcast(BF16).rearrange(
+                in_=x_t[p][:].rearrange("q u b -> q (u b)").bitcast(BF16).rearrange(
                     "q (u b e) -> q b u e", u=WORDS, e=PAIR
                 ),
                 func=ACT.Identity,
@@ -84,13 +89,12 @@ def tile_better_transformer_s_kernel(tc, x, weights, bias, gain, norm_bias, gamm
                 scale=gain_f32[:],
             )
 
-        def regroup_w(p):
-            for h in range(W_PIECES):
-                cols = slice(h * D // W_PIECES, (h + 1) * D // W_PIECES)
-                nc.vector.tensor_copy(
-                    out=w_grouped[p][:, cols, :].rearrange("q (c r) t -> q c t r", r=4),
-                    in_=w_raw[p][:, :, cols].rearrange("q t (c r) -> q c t r", r=4),
-                )
+        def regroup_w(copy, p, first, last):
+            cols = slice(first, last)
+            copy(
+                out=w_grouped[p][:, cols, :].rearrange("q (c r) t -> q c t r", r=4),
+                in_=w_raw[p][:, :, cols].rearrange("q t (c r) -> q c t r", r=4),
+            )
 
         def quantise_w(p):
             for h in range(W_PIECES):
@@ -134,8 +138,7 @@ def tile_better_transformer_s_kernel(tc, x, weights, bias, gain, norm_bias, gamm
                 out=sig[:], in_=y_t[j][:], func=ACT.Sigmoid, bias=beta_bias_col[:, col], scale=beta_col[:, col]
             )
             mult = work.tile([P, BATCH], F32, tag="mult")
-            mult_engine = nc.vector if j < COL_TILES else nc.gpsimd
-            mult_engine.tensor_scalar(
+            nc.gpsimd.tensor_scalar(
                 out=mult[:], in0=sig[:], scalar1=rest_col[:, col], scalar2=gamma_col[:, col],
                 op0=ALU.mult, op1=ALU.add,
             )
@@ -162,37 +165,43 @@ def tile_better_transformer_s_kernel(tc, x, weights, bias, gain, norm_bias, gamm
                 out=out[:, g * width : (g + 1) * width].rearrange("(i b) c -> b i c", b=P), in_=result[:]
             )
 
+        half = D // W_PIECES
+        nc.gpsimd.memset(vec_rows[:], 0.0)
+        nc.gpsimd.memset(warm_in[:], 0.0)
         with nc.allow_non_contiguous_dma(reason="one bfloat16 number to each partition"):
             nc.scalar.dma_start(out=gain_bf[:], in_=gain.partition_broadcast(P))
             nc.scalar.dma_start(out=shift_bf[:], in_=norm_bias.partition_broadcast(P))
         load_part(0)
-        nc.vector.memset(vec_rows[:], 0.0)
         for r, vec in enumerate((bias, gamma, beta)):
             nc.scalar.dma_start(
                 out=vec_rows[r * n_tiles : (r + 1) * n_tiles, :], in_=vec.rearrange("(j c) -> j c", c=P)
             )
         load_part(1)
 
-        nc.vector.memset(warm_in[:], 0.0)
         nc.scalar.activation(out=warm_out[:], in_=warm_in[:], func=ACT.Sigmoid)
         masks.make_identity(nc, ident_f32[:])
         masks.make_identity(nc, ident_bf[:])
-        nc.vector.tensor_copy(out=gain_f32[:], in_=gain_bf[:])
-        nc.vector.tensor_copy(out=shift_f32[:], in_=shift_bf[:])
+        nc.gpsimd.tensor_copy(out=gain_f32[:], in_=gain_bf[:])
+        nc.gpsimd.tensor_copy(out=shift_f32[:], in_=shift_bf[:])
 
-        regroup_w(0)
-        normalise_x(0)
+        regroup_w(nc.vector.tensor_copy, 0, 0, half)
+        regroup_w(nc.vector.tensor_copy, 0, half, D - S_COLS)
+        regroup_w(nc.scalar.copy, 0, D - S_COLS, D)
+        x_transposes(0)
         quantise_w(0)
 
         vec_t = psum.tile([P, P], BF16, tag="bank")
         nc.tensor.transpose(vec_t[:], vec_rows[:], ident_bf[:])
-        nc.vector.tensor_copy(out=vec_cols[:], in_=vec_t[:, 0 : 3 * n_tiles])
-        nc.vector.tensor_mul(out=beta_bias_col[:], in0=beta_col, in1=bias_col)
-        nc.vector.tensor_scalar(
+        nc.scalar.copy(out=vec_cols[:], in_=vec_t[:, 0 : 3 * n_tiles])
+        nc.gpsimd.tensor_tensor(out=beta_bias_col[:], in0=beta_col, in1=bias_col, op=ALU.mult)
+        nc.gpsimd.tensor_scalar(
             out=rest_col[:], in0=gamma_col, scalar1=-1.0, scalar2=1.0, op0=ALU.mult, op1=ALU.add
         )
 
-        regroup_w(1)
+        normalise_x(0)
+        regroup_w(nc.vector.tensor_copy, 1, 0, half)
+        regroup_w(nc.vector.tensor_copy, 1, half, D)
+        x_transposes(1)
         normalise_x(1)
         quantise_x(0)
         multiply(0)

@@ -22,6 +22,7 @@ PAIR = 2
 WORDS = PACK // PAIR
 W_PIECES = 2
 JOINT = 2
+PE_RESIDUAL = (2,)
 S_COLS = 192
 
 FLOPS = 2 * BATCH * PARTS * D * D
@@ -130,37 +131,61 @@ def tile_better_transformer_s_kernel(tc, x, weights, bias, gain, norm_bias, gamm
                 y_t.append(acc)
 
         back = {}
+        sig = {}
+        mult = {}
 
-        def activate(j):
+        def sigmoid(j):
             col = slice(j, j + 1)
-            sig = work.tile([P, BATCH], F32, tag="sig")
+            sig[j] = work.tile([P, BATCH], F32, tag="sig", name="sig%d" % j)
             nc.scalar.activation(
-                out=sig[:], in_=y_t[j][:], func=ACT.Sigmoid, bias=beta_bias_col[:, col], scale=beta_col[:, col]
+                out=sig[j][:], in_=y_t[j][:], func=ACT.Sigmoid, bias=beta_bias_col[:, col], scale=beta_col[:, col]
             )
-            mult = work.tile([P, BATCH], F32, tag="mult")
-            nc.gpsimd.tensor_scalar(
-                out=mult[:], in0=sig[:], scalar1=rest_col[:, col], scalar2=gamma_col[:, col],
-                op0=ALU.mult, op1=ALU.add,
-            )
+
+        def multiplier(j):
+            col = slice(j, j + 1)
+            mult[j] = work.tile([P, BATCH], F32, tag="mult", name="mult%d" % j)
+            if j % 2 == 1:
+                nc.scalar.activation(
+                    out=mult[j][:], in_=sig[j][:], func=ACT.Identity, bias=gamma_col[:, col], scale=rest_col[:, col]
+                )
+            else:
+                nc.gpsimd.tensor_scalar(
+                    out=mult[j][:], in0=sig[j][:], scalar1=rest_col[:, col], scalar2=gamma_col[:, col],
+                    op0=ALU.mult, op1=ALU.add,
+                )
+
+        def product(j):
+            col = slice(j, j + 1)
             act_t = work.tile([P, BATCH], F32, tag="act_t")
             nc.vector.scalar_tensor_tensor(
-                out=act_t[:], in0=y_t[j][:], scalar=bias_col[:, col], in1=mult[:], op0=ALU.add, op1=ALU.mult
+                out=act_t[:], in0=y_t[j][:], scalar=bias_col[:, col], in1=mult[j][:], op0=ALU.add, op1=ALU.mult
             )
             g = j // JOINT
             place = j % JOINT
             if place == 0:
                 back[g] = psum.tile([P, ROW_TILES, JOINT * P], F32, tag="bank", name="back%d" % g)
+            p = j // COL_TILES
+            in_part = slice(j * P - p * D, (j + 1) * P - p * D)
             for i in range(ROW_TILES):
-                nc.tensor.transpose(
-                    back[g][:, i, place * P : (place + 1) * P], act_t[:, i * P : (i + 1) * P], ident_f32[:]
-                )
+                block = back[g][:, i, place * P : (place + 1) * P]
+                if g in PE_RESIDUAL:
+                    nc.tensor.matmul(block, lhsT=ident_bf[:], rhs=x_raw[p][:, i, in_part], start=True, stop=False)
+                    nc.tensor.matmul(
+                        block, lhsT=act_t[:, i * P : (i + 1) * P], rhs=ident_f32[:], is_transpose=True,
+                        start=False, stop=True,
+                    )
+                else:
+                    nc.tensor.transpose(block, act_t[:, i * P : (i + 1) * P], ident_f32[:])
 
         def add_residual_and_store(g):
             width = JOINT * P
             p = g * width // D
             in_part = slice(g * width - p * D, (g + 1) * width - p * D)
             result = work.tile([P, ROW_TILES, width], F32, tag="result")
-            nc.vector.tensor_tensor(out=result[:], in0=back[g][:], in1=x_raw[p][:, :, in_part], op=ALU.add)
+            if g in PE_RESIDUAL:
+                nc.scalar.copy(out=result[:], in_=back[g][:])
+            else:
+                nc.vector.tensor_tensor(out=result[:], in0=back[g][:], in1=x_raw[p][:, :, in_part], op=ALU.add)
             nc.sync.dma_start(
                 out=out[:, g * width : (g + 1) * width].rearrange("(i b) c -> b i c", b=P), in_=result[:]
             )
@@ -209,8 +234,15 @@ def tile_better_transformer_s_kernel(tc, x, weights, bias, gain, norm_bias, gamm
         quantise_x(1)
         multiply(1)
 
-        for j in range(n_tiles):
-            activate(j)
-            if j % JOINT == JOINT - 1 and j >= 2 * JOINT - 1:
-                add_residual_and_store(j // JOINT - 1)
-        add_residual_and_store(n_tiles // JOINT - 1)
+        for step in range(n_tiles + 2):
+            if step < n_tiles:
+                sigmoid(step)
+            if 0 <= step - 1 < n_tiles:
+                multiplier(step - 1)
+            j = step - 2
+            if j >= 0:
+                product(j)
+                if j == 2 * JOINT - 1:
+                    add_residual_and_store(0)
+        for g in range(1, n_tiles // JOINT):
+            add_residual_and_store(g)

@@ -23,6 +23,7 @@ WORDS = PACK // PAIR
 W_PIECES = 2
 JOINT = 2
 PE_RESIDUAL = (2,)
+V_MULTS = 2
 S_COLS = 192
 
 FLOPS = 2 * BATCH * PARTS * D * D
@@ -70,19 +71,18 @@ def tile_better_transformer_s_kernel(tc, x, weights, bias, gain, norm_bias, gamm
 
         x_t = {}
 
-        def x_transposes(p):
+        def x_transposes(p, i):
             x_words = x_raw[p][:].rearrange("b i k -> b (i k)").bitcast(F32).rearrange(
                 "b (i q u) -> b i u q", i=ROW_TILES, u=WORDS
             )
-            x_t[p] = psum.tile([P, WORDS, BATCH], F32, tag="bank", name="x_t%d" % p)
-            for i in range(ROW_TILES):
-                for u in range(WORDS):
-                    nc.tensor.transpose(x_t[p][:, u, i * P : (i + 1) * P], x_words[:, i, u, :], ident_f32[:])
+            x_t[p, i] = psum.tile([P, WORDS, P], F32, tag="bank", name="x_t%d_%d" % (p, i))
+            for u in range(WORDS):
+                nc.tensor.transpose(x_t[p, i][:, u, :], x_words[:, i, u, :], ident_f32[:])
 
-        def normalise_x(p):
+        def normalise_x(p, i):
             nc.scalar.activation(
-                out=x_grouped[p][:].rearrange("q b (u e) -> q b u e", u=WORDS),
-                in_=x_t[p][:].rearrange("q u b -> q (u b)").bitcast(BF16).rearrange(
+                out=x_grouped[p][:, i * P : (i + 1) * P, :].rearrange("q b (u e) -> q b u e", u=WORDS),
+                in_=x_t[p, i][:].rearrange("q u b -> q (u b)").bitcast(BF16).rearrange(
                     "q (u b e) -> q b u e", u=WORDS, e=PAIR
                 ),
                 func=ACT.Identity,
@@ -144,12 +144,13 @@ def tile_better_transformer_s_kernel(tc, x, weights, bias, gain, norm_bias, gamm
         def multiplier(j):
             col = slice(j, j + 1)
             mult[j] = work.tile([P, BATCH], F32, tag="mult", name="mult%d" % j)
-            if j % 2 == 1:
+            if j >= V_MULTS and j % 2 == 1:
                 nc.scalar.activation(
                     out=mult[j][:], in_=sig[j][:], func=ACT.Identity, bias=gamma_col[:, col], scale=rest_col[:, col]
                 )
             else:
-                nc.gpsimd.tensor_scalar(
+                engine = nc.vector if j < V_MULTS else nc.gpsimd
+                engine.tensor_scalar(
                     out=mult[j][:], in0=sig[j][:], scalar1=rest_col[:, col], scalar2=gamma_col[:, col],
                     op0=ALU.mult, op1=ALU.add,
                 )
@@ -212,22 +213,25 @@ def tile_better_transformer_s_kernel(tc, x, weights, bias, gain, norm_bias, gamm
         regroup_w(nc.vector.tensor_copy, 0, 0, half)
         regroup_w(nc.vector.tensor_copy, 0, half, D - S_COLS)
         regroup_w(nc.scalar.copy, 0, D - S_COLS, D)
-        x_transposes(0)
-        quantise_w(0)
-
+        x_transposes(0, 0)
         vec_t = psum.tile([P, P], BF16, tag="bank")
         nc.tensor.transpose(vec_t[:], vec_rows[:], ident_bf[:])
+        x_transposes(0, 1)
+        quantise_w(0)
+
+        normalise_x(0, 0)
         nc.scalar.copy(out=vec_cols[:], in_=vec_t[:, 0 : 3 * n_tiles])
         nc.gpsimd.tensor_tensor(out=beta_bias_col[:], in0=beta_col, in1=bias_col, op=ALU.mult)
         nc.gpsimd.tensor_scalar(
             out=rest_col[:], in0=gamma_col, scalar1=-1.0, scalar2=1.0, op0=ALU.mult, op1=ALU.add
         )
+        normalise_x(0, 1)
 
-        normalise_x(0)
         regroup_w(nc.vector.tensor_copy, 1, 0, half)
         regroup_w(nc.vector.tensor_copy, 1, half, D)
-        x_transposes(1)
-        normalise_x(1)
+        for i in range(ROW_TILES):
+            x_transposes(1, i)
+            normalise_x(1, i)
         quantise_x(0)
         multiply(0)
         quantise_w(1)

@@ -21,8 +21,8 @@ COL_TILES = D // P
 PAIR = 2
 WORDS = PACK // PAIR
 W_PIECES = 2
-JOINT = 2
-PE_RESIDUAL = (2,)
+GROUPS = ((0, 1), (2, 3), (4,), (5, 6), (7,))
+PE_RESIDUAL = (1, 2)
 V_MULTS = 2
 S_COLS = 192
 
@@ -161,10 +161,10 @@ def tile_better_transformer_s_kernel(tc, x, weights, bias, gain, norm_bias, gamm
             nc.vector.scalar_tensor_tensor(
                 out=act_t[:], in0=y_t[j][:], scalar=bias_col[:, col], in1=mult[j][:], op0=ALU.add, op1=ALU.mult
             )
-            g = j // JOINT
-            place = j % JOINT
+            g = [n for n in range(len(GROUPS)) if j in GROUPS[n]][0]
+            place = GROUPS[g].index(j)
             if place == 0:
-                back[g] = psum.tile([P, ROW_TILES, JOINT * P], F32, tag="bank", name="back%d" % g)
+                back[g] = psum.tile([P, ROW_TILES, len(GROUPS[g]) * P], F32, tag="bank", name="back%d" % g)
             p = j // COL_TILES
             in_part = slice(j * P - p * D, (j + 1) * P - p * D)
             for i in range(ROW_TILES):
@@ -179,17 +179,19 @@ def tile_better_transformer_s_kernel(tc, x, weights, bias, gain, norm_bias, gamm
                     nc.tensor.transpose(block, act_t[:, i * P : (i + 1) * P], ident_f32[:])
 
         def add_residual_and_store(g):
-            width = JOINT * P
-            p = g * width // D
-            in_part = slice(g * width - p * D, (g + 1) * width - p * D)
-            result = work.tile([P, ROW_TILES, width], F32, tag="result")
+            first = GROUPS[g][0] * P
+            width = len(GROUPS[g]) * P
+            p = first // D
+            result = parts.tile([P, ROW_TILES, width], F32, name="result%d" % g)
             if g in PE_RESIDUAL:
                 nc.scalar.copy(out=result[:], in_=back[g][:])
+                queue = nc.scalar
             else:
-                nc.vector.tensor_tensor(out=result[:], in0=back[g][:], in1=x_raw[p][:, :, in_part], op=ALU.add)
-            nc.sync.dma_start(
-                out=out[:, g * width : (g + 1) * width].rearrange("(i b) c -> b i c", b=P), in_=result[:]
-            )
+                nc.vector.tensor_tensor(
+                    out=result[:], in0=back[g][:], in1=x_raw[p][:, :, first - p * D : first - p * D + width], op=ALU.add
+                )
+                queue = nc.sync
+            queue.dma_start(out=out[:, first : first + width].rearrange("(i b) c -> b i c", b=P), in_=result[:])
 
         half = D // W_PIECES
         nc.gpsimd.memset(vec_rows[:], 0.0)
@@ -246,7 +248,7 @@ def tile_better_transformer_s_kernel(tc, x, weights, bias, gain, norm_bias, gamm
             j = step - 2
             if j >= 0:
                 product(j)
-                if j == 2 * JOINT - 1:
+                if j == GROUPS[1][-1]:
                     add_residual_and_store(0)
-        for g in range(1, n_tiles // JOINT):
+        for g in range(1, len(GROUPS)):
             add_residual_and_store(g)

@@ -209,12 +209,12 @@ def tile_better_transformer_s_kernel(tc, x, weights, bias, gain, norm_bias, gamm
         nc.scalar.activation(out=warm_out[:], in_=warm_in[:], func=ACT.Sigmoid)
         masks.make_identity(nc, ident_f32[:])
         masks.make_identity(nc, ident_bf[:])
-        nc.gpsimd.tensor_copy(out=gain_f32[:], in_=gain_bf[:])
-        nc.gpsimd.tensor_copy(out=shift_f32[:], in_=shift_bf[:])
 
         regroup_w(nc.vector.tensor_copy, 0, 0, half)
         regroup_w(nc.vector.tensor_copy, 0, half, D - S_COLS)
         regroup_w(nc.scalar.copy, 0, D - S_COLS, D)
+        nc.scalar.copy(out=gain_f32[:], in_=gain_bf[:])
+        nc.scalar.copy(out=shift_f32[:], in_=shift_bf[:])
         x_transposes(0, 0)
         vec_t = psum.tile([P, P], BF16, tag="bank")
         nc.tensor.transpose(vec_t[:], vec_rows[:], ident_bf[:])

@@ -65,9 +65,13 @@ def tile_better_transformer_s_kernel(tc, x, weights, bias, gain, norm_bias, gamm
 
         def load_part(p):
             nc.sync.dma_start(out=w_raw[p][:], in_=weights[p].rearrange("(q t) c -> q t c", t=PACK))
-            nc.sync.dma_start(
-                out=x_raw[p][:], in_=x[:, p * D : (p + 1) * D].rearrange("(i b) k -> b i k", b=P)
-            )
+            if p < PARTS - 1:
+                nc.sync.dma_start(
+                    out=x_raw[p][:], in_=x[:, p * D : (p + 1) * D].rearrange("(i b) k -> b i k", b=P)
+                )
+            else:
+                for i in range(ROW_TILES):
+                    nc.sync.dma_start(out=x_raw[p][:, i, :], in_=x[i * P : (i + 1) * P, p * D : (p + 1) * D])
 
         x_t = {}
 
@@ -200,11 +204,11 @@ def tile_better_transformer_s_kernel(tc, x, weights, bias, gain, norm_bias, gamm
             nc.scalar.dma_start(out=gain_bf[:], in_=gain.partition_broadcast(P))
             nc.scalar.dma_start(out=shift_bf[:], in_=norm_bias.partition_broadcast(P))
         load_part(0)
+        load_part(1)
         for r, vec in enumerate((bias, gamma, beta)):
             nc.scalar.dma_start(
                 out=vec_rows[r * n_tiles : (r + 1) * n_tiles, :], in_=vec.rearrange("(j c) -> j c", c=P)
             )
-        load_part(1)
 
         nc.scalar.activation(out=warm_out[:], in_=warm_in[:], func=ACT.Sigmoid)
         masks.make_identity(nc, ident_f32[:])
@@ -216,18 +220,18 @@ def tile_better_transformer_s_kernel(tc, x, weights, bias, gain, norm_bias, gamm
         nc.scalar.copy(out=gain_f32[:], in_=gain_bf[:])
         nc.scalar.copy(out=shift_f32[:], in_=shift_bf[:])
         x_transposes(0, 0)
-        vec_t = psum.tile([P, P], BF16, tag="bank")
-        nc.tensor.transpose(vec_t[:], vec_rows[:], ident_bf[:])
         x_transposes(0, 1)
         quantise_w(0)
-
         normalise_x(0, 0)
+        normalise_x(0, 1)
+
+        vec_t = psum.tile([P, P], BF16, tag="bank")
+        nc.tensor.transpose(vec_t[:], vec_rows[:], ident_bf[:])
         nc.scalar.copy(out=vec_cols[:], in_=vec_t[:, 0 : 3 * n_tiles])
         nc.gpsimd.tensor_tensor(out=beta_bias_col[:], in0=beta_col, in1=bias_col, op=ALU.mult)
         nc.gpsimd.tensor_scalar(
             out=rest_col[:], in0=gamma_col, scalar1=-1.0, scalar2=1.0, op0=ALU.mult, op1=ALU.add
         )
-        normalise_x(0, 1)
 
         regroup_w(nc.vector.tensor_copy, 1, 0, half)
         regroup_w(nc.vector.tensor_copy, 1, half, D)

@@ -21,10 +21,10 @@ COL_TILES = D // P
 PAIR = 2
 WORDS = PACK // PAIR
 W_PIECES = 2
-GROUPS = ((0, 1), (2, 3), (4,), (5, 6), (7,))
-PE_RESIDUAL = (1, 2)
-V_MULTS = 2
-S_COLS = 192
+GROUPS = ((0,), (1, 2), (3, 4), (5,), (6,), (7,))
+PE_RESIDUAL = (0, 2)
+MULT_ENGINE = ("V", "V", "S", "G", "V", "G", "G", "S")
+S_COLS = 128
 
 FLOPS = 2 * BATCH * PARTS * D * D
 
@@ -35,7 +35,7 @@ def tile_better_transformer_s_kernel(tc, x, weights, bias, gain, norm_bias, gamm
     with ExitStack() as ctx:
         consts = ctx.enter_context(tc.tile_pool(name="consts", bufs=1))
         parts = ctx.enter_context(tc.tile_pool(name="parts", bufs=1))
-        work = ctx.enter_context(tc.tile_pool(name="work", bufs=4))
+        work = ctx.enter_context(tc.tile_pool(name="work", bufs=8))
         psum = ctx.enter_context(tc.psum_pool(name="psum", bufs=8))
         ctx.enter_context(tc.manual_schedule())
 
@@ -83,16 +83,17 @@ def tile_better_transformer_s_kernel(tc, x, weights, bias, gain, norm_bias, gamm
             for u in range(WORDS):
                 nc.tensor.transpose(x_t[p, i][:, u, :], x_words[:, i, u, :], ident_f32[:])
 
-        def normalise_x(p, i):
-            nc.scalar.activation(
-                out=x_grouped[p][:, i * P : (i + 1) * P, :].rearrange("q b (u e) -> q b u e", u=WORDS),
-                in_=x_t[p, i][:].rearrange("q u b -> q (u b)").bitcast(BF16).rearrange(
-                    "q (u b e) -> q b u e", u=WORDS, e=PAIR
-                ),
-                func=ACT.Identity,
-                bias=shift_f32[:],
-                scale=gain_f32[:],
+        def normalise_x(engine, p, i):
+            grouped = x_grouped[p][:, i * P : (i + 1) * P, :].rearrange("q b (u e) -> q b u e", u=WORDS)
+            pairs = x_t[p, i][:].rearrange("q u b -> q (u b)").bitcast(BF16).rearrange(
+                "q (u b e) -> q b u e", u=WORDS, e=PAIR
             )
+            if engine == "S":
+                nc.scalar.activation(out=grouped, in_=pairs, func=ACT.Identity, bias=shift_f32[:], scale=gain_f32[:])
+            else:
+                nc.vector.tensor_scalar(
+                    out=grouped, in0=pairs, scalar1=gain_f32[:], scalar2=shift_f32[:], op0=ALU.mult, op1=ALU.add
+                )
 
         def regroup_w(copy, p, first, last):
             cols = slice(first, last)
@@ -101,14 +102,13 @@ def tile_better_transformer_s_kernel(tc, x, weights, bias, gain, norm_bias, gamm
                 in_=w_raw[p][:, :, cols].rearrange("q t (c r) -> q c t r", r=4),
             )
 
-        def quantise_w(p):
-            for h in range(W_PIECES):
-                cols = slice(h * D // W_PIECES, (h + 1) * D // W_PIECES)
-                nc.vector.quantize_mx(
-                    out=w_codes[p][:, cols].bitcast(FP8X4),
-                    scales=w_scales[p][:, cols],
-                    in_=w_grouped[p][:, cols, :].rearrange("q c t -> q (c t)"),
-                )
+        def quantise_w(p, h):
+            cols = slice(h * D // W_PIECES, (h + 1) * D // W_PIECES)
+            nc.vector.quantize_mx(
+                out=w_codes[p][:, cols].bitcast(FP8X4),
+                scales=w_scales[p][:, cols],
+                in_=w_grouped[p][:, cols, :].rearrange("q c t -> q (c t)"),
+            )
 
         def quantise_x(p):
             nc.vector.quantize_mx(
@@ -148,12 +148,12 @@ def tile_better_transformer_s_kernel(tc, x, weights, bias, gain, norm_bias, gamm
         def multiplier(j):
             col = slice(j, j + 1)
             mult[j] = work.tile([P, BATCH], F32, tag="mult", name="mult%d" % j)
-            if j >= V_MULTS and j % 2 == 1:
+            if MULT_ENGINE[j] == "S":
                 nc.scalar.activation(
                     out=mult[j][:], in_=sig[j][:], func=ACT.Identity, bias=gamma_col[:, col], scale=rest_col[:, col]
                 )
             else:
-                engine = nc.vector if j < V_MULTS else nc.gpsimd
+                engine = nc.vector if MULT_ENGINE[j] == "V" else nc.gpsimd
                 engine.tensor_scalar(
                     out=mult[j][:], in0=sig[j][:], scalar1=rest_col[:, col], scalar2=gamma_col[:, col],
                     op0=ALU.mult, op1=ALU.add,
@@ -189,7 +189,7 @@ def tile_better_transformer_s_kernel(tc, x, weights, bias, gain, norm_bias, gamm
             result = parts.tile([P, ROW_TILES, width], F32, name="result%d" % g)
             if g in PE_RESIDUAL:
                 nc.scalar.copy(out=result[:], in_=back[g][:])
-                queue = nc.scalar
+                queue = nc.scalar if g == PE_RESIDUAL[-1] else nc.sync
             else:
                 nc.vector.tensor_tensor(
                     out=result[:], in0=back[g][:], in1=x_raw[p][:, :, first - p * D : first - p * D + width], op=ALU.add
@@ -221,9 +221,10 @@ def tile_better_transformer_s_kernel(tc, x, weights, bias, gain, norm_bias, gamm
         nc.scalar.copy(out=shift_f32[:], in_=shift_bf[:])
         x_transposes(0, 0)
         x_transposes(0, 1)
-        quantise_w(0)
-        normalise_x(0, 0)
-        normalise_x(0, 1)
+        quantise_w(0, 0)
+        quantise_w(0, 1)
+        normalise_x("S", 0, 0)
+        normalise_x("S", 0, 1)
 
         vec_t = psum.tile([P, P], BF16, tag="bank")
         nc.tensor.transpose(vec_t[:], vec_rows[:], ident_bf[:])
@@ -233,26 +234,45 @@ def tile_better_transformer_s_kernel(tc, x, weights, bias, gain, norm_bias, gamm
             out=rest_col[:], in0=gamma_col, scalar1=-1.0, scalar2=1.0, op0=ALU.mult, op1=ALU.add
         )
 
+        regroup_w(nc.scalar.copy, 1, D - S_COLS, D)
         regroup_w(nc.vector.tensor_copy, 1, 0, half)
-        regroup_w(nc.vector.tensor_copy, 1, half, D)
-        for i in range(ROW_TILES):
-            x_transposes(1, i)
-            normalise_x(1, i)
+        regroup_w(nc.vector.tensor_copy, 1, half, D - S_COLS)
+        x_transposes(1, 0)
+        x_transposes(1, 1)
         quantise_x(0)
+        normalise_x("S", 1, 0)
+        normalise_x("V", 1, 1)
         multiply(0)
-        quantise_w(1)
+        quantise_w(1, 0)
         quantise_x(1)
+        quantise_w(1, 1)
         multiply(1)
 
-        for step in range(n_tiles + 2):
-            if step < n_tiles:
-                sigmoid(step)
-            if 0 <= step - 1 < n_tiles:
-                multiplier(step - 1)
-            j = step - 2
-            if j >= 0:
-                product(j)
-                if j == GROUPS[1][-1]:
-                    add_residual_and_store(0)
-        for g in range(1, len(GROUPS)):
+        sigmoid(0)
+        sigmoid(1)
+        multiplier(0)
+        multiplier(1)
+        sigmoid(2)
+        sigmoid(3)
+        multiplier(3)
+        multiplier(2)
+        product(0)
+        product(1)
+        sigmoid(4)
+        product(2)
+        multiplier(4)
+        product(3)
+        sigmoid(5)
+        multiplier(5)
+        product(4)
+        sigmoid(6)
+        multiplier(6)
+        sigmoid(7)
+        add_residual_and_store(1)
+        add_residual_and_store(0)
+        multiplier(7)
+        product(5)
+        product(6)
+        product(7)
+        for g in range(2, len(GROUPS)):
             add_residual_and_store(g)

@@ -21,9 +21,9 @@ COL_TILES = D // P
 PAIR = 2
 WORDS = PACK // PAIR
 W_PIECES = 2
-GROUPS = ((0,), (1, 2), (3, 4), (5,), (6,), (7,))
-PE_RESIDUAL = (0, 2)
-MULT_ENGINE = ("V", "V", "S", "G", "V", "G", "G", "S")
+PIECES = ((0, (0, 1)), (2, (0, 1)), (4, (0,)), (4, (1,)), (6, (0,)), (6, (1,)))
+PE_RESIDUAL = (1, 2)
+MULT_ENGINE = ("V", "V", "S", "G", "S", "G", "G", "S")
 S_COLS = 128
 
 FLOPS = 2 * BATCH * PARTS * D * D
@@ -63,15 +63,12 @@ def tile_better_transformer_s_kernel(tc, x, weights, bias, gain, norm_bias, gamm
         ident_f32 = consts.tile([P, P], F32)
         ident_bf = consts.tile([P, P], BF16)
 
-        def load_part(p):
+        def load_part_weights(p):
             nc.sync.dma_start(out=w_raw[p][:], in_=weights[p].rearrange("(q t) c -> q t c", t=PACK))
-            if p < PARTS - 1:
-                nc.sync.dma_start(
-                    out=x_raw[p][:], in_=x[:, p * D : (p + 1) * D].rearrange("(i b) k -> b i k", b=P)
-                )
-            else:
-                for i in range(ROW_TILES):
-                    nc.sync.dma_start(out=x_raw[p][:, i, :], in_=x[i * P : (i + 1) * P, p * D : (p + 1) * D])
+
+        def load_part_x(p):
+            for i in range(ROW_TILES):
+                nc.sync.dma_start(out=x_raw[p][:, i, :], in_=x[i * P : (i + 1) * P, p * D : (p + 1) * D])
 
         x_t = {}
 
@@ -165,37 +162,42 @@ def tile_better_transformer_s_kernel(tc, x, weights, bias, gain, norm_bias, gamm
             nc.vector.scalar_tensor_tensor(
                 out=act_t[:], in0=y_t[j][:], scalar=bias_col[:, col], in1=mult[j][:], op0=ALU.add, op1=ALU.mult
             )
-            g = [n for n in range(len(GROUPS)) if j in GROUPS[n]][0]
-            place = GROUPS[g].index(j)
-            if place == 0:
-                back[g] = psum.tile([P, ROW_TILES, len(GROUPS[g]) * P], F32, tag="bank", name="back%d" % g)
             p = j // COL_TILES
             in_part = slice(j * P - p * D, (j + 1) * P - p * D)
-            for i in range(ROW_TILES):
-                block = back[g][:, i, place * P : (place + 1) * P]
-                if g in PE_RESIDUAL:
-                    nc.tensor.matmul(block, lhsT=ident_bf[:], rhs=x_raw[p][:, i, in_part], start=True, stop=False)
-                    nc.tensor.matmul(
-                        block, lhsT=act_t[:, i * P : (i + 1) * P], rhs=ident_f32[:], is_transpose=True,
-                        start=False, stop=True,
-                    )
-                else:
-                    nc.tensor.transpose(block, act_t[:, i * P : (i + 1) * P], ident_f32[:])
+            place = j % 2
+            for n, (first, rows) in enumerate(PIECES):
+                if j - place != first:
+                    continue
+                if place == 0:
+                    back[n] = psum.tile([P, len(rows), 2 * P], F32, tag="bank", name="back%d" % n)
+                for r, i in enumerate(rows):
+                    block = back[n][:, r, place * P : (place + 1) * P]
+                    if n in PE_RESIDUAL:
+                        nc.tensor.matmul(block, lhsT=ident_bf[:], rhs=x_raw[p][:, i, in_part], start=True, stop=False)
+                        nc.tensor.matmul(
+                            block, lhsT=act_t[:, i * P : (i + 1) * P], rhs=ident_f32[:], is_transpose=True,
+                            start=False, stop=True,
+                        )
+                    else:
+                        nc.tensor.transpose(block, act_t[:, i * P : (i + 1) * P], ident_f32[:])
 
-        def add_residual_and_store(g):
-            first = GROUPS[g][0] * P
-            width = len(GROUPS[g]) * P
-            p = first // D
-            result = parts.tile([P, ROW_TILES, width], F32, name="result%d" % g)
-            if g in PE_RESIDUAL:
-                nc.scalar.copy(out=result[:], in_=back[g][:])
-                queue = nc.scalar if g == PE_RESIDUAL[-1] else nc.sync
+        def add_residual_and_store(n):
+            first, rows = PIECES[n]
+            p = first // COL_TILES
+            cols = slice(first * P, (first + 2) * P)
+            in_part = slice(first * P - p * D, (first + 2) * P - p * D)
+            result = parts.tile([P, len(rows), 2 * P], F32, name="result%d" % n)
+            if n in PE_RESIDUAL:
+                nc.scalar.copy(out=result[:], in_=back[n][:])
+                queue = nc.scalar if n == PE_RESIDUAL[-1] else nc.sync
             else:
                 nc.vector.tensor_tensor(
-                    out=result[:], in0=back[g][:], in1=x_raw[p][:, :, first - p * D : first - p * D + width], op=ALU.add
+                    out=result[:], in0=back[n][:], in1=x_raw[p][:, rows[0] : rows[-1] + 1, in_part], op=ALU.add
                 )
                 queue = nc.sync
-            queue.dma_start(out=out[:, first : first + width].rearrange("(i b) c -> b i c", b=P), in_=result[:])
+            queue.dma_start(
+                out=out[rows[0] * P : (rows[-1] + 1) * P, cols].rearrange("(i b) c -> b i c", b=P), in_=result[:]
+            )
 
         half = D // W_PIECES
         nc.gpsimd.memset(vec_rows[:], 0.0)
@@ -203,12 +205,14 @@ def tile_better_transformer_s_kernel(tc, x, weights, bias, gain, norm_bias, gamm
         with nc.allow_non_contiguous_dma(reason="one bfloat16 number to each partition"):
             nc.scalar.dma_start(out=gain_bf[:], in_=gain.partition_broadcast(P))
             nc.scalar.dma_start(out=shift_bf[:], in_=norm_bias.partition_broadcast(P))
-        load_part(0)
-        load_part(1)
+        load_part_weights(0)
+        load_part_x(0)
+        load_part_weights(1)
         for r, vec in enumerate((bias, gamma, beta)):
-            nc.scalar.dma_start(
+            nc.sync.dma_start(
                 out=vec_rows[r * n_tiles : (r + 1) * n_tiles, :], in_=vec.rearrange("(j c) -> j c", c=P)
             )
+        load_part_x(1)
 
         nc.scalar.activation(out=warm_out[:], in_=warm_in[:], func=ACT.Sigmoid)
         masks.make_identity(nc, ident_f32[:])
@@ -260,19 +264,19 @@ def tile_better_transformer_s_kernel(tc, x, weights, bias, gain, norm_bias, gamm
         product(1)
         sigmoid(4)
         product(2)
-        multiplier(4)
         product(3)
         sigmoid(5)
+        multiplier(4)
         multiplier(5)
-        product(4)
+        add_residual_and_store(0)
         sigmoid(6)
         multiplier(6)
+        product(4)
         sigmoid(7)
-        add_residual_and_store(1)
-        add_residual_and_store(0)
         multiplier(7)
+        add_residual_and_store(1)
         product(5)
         product(6)
         product(7)
-        for g in range(2, len(GROUPS)):
-            add_residual_and_store(g)
+        for n in range(2, len(PIECES)):
+            add_residual_and_store(n)

@@ -63,12 +63,15 @@ def tile_better_transformer_s_kernel(tc, x, weights, bias, gain, norm_bias, gamm
         ident_f32 = consts.tile([P, P], F32)
         ident_bf = consts.tile([P, P], BF16)
 
-        def load_part_weights(p):
+        def load_part(p):
             nc.sync.dma_start(out=w_raw[p][:], in_=weights[p].rearrange("(q t) c -> q t c", t=PACK))
-
-        def load_part_x(p):
-            for i in range(ROW_TILES):
-                nc.sync.dma_start(out=x_raw[p][:, i, :], in_=x[i * P : (i + 1) * P, p * D : (p + 1) * D])
+            if p < PARTS - 1:
+                nc.sync.dma_start(
+                    out=x_raw[p][:], in_=x[:, p * D : (p + 1) * D].rearrange("(i b) k -> b i k", b=P)
+                )
+            else:
+                for i in range(ROW_TILES):
+                    nc.sync.dma_start(out=x_raw[p][:, i, :], in_=x[i * P : (i + 1) * P, p * D : (p + 1) * D])
 
         x_t = {}
 
@@ -205,14 +208,12 @@ def tile_better_transformer_s_kernel(tc, x, weights, bias, gain, norm_bias, gamm
         with nc.allow_non_contiguous_dma(reason="one bfloat16 number to each partition"):
             nc.scalar.dma_start(out=gain_bf[:], in_=gain.partition_broadcast(P))
             nc.scalar.dma_start(out=shift_bf[:], in_=norm_bias.partition_broadcast(P))
-        load_part_weights(0)
-        load_part_x(0)
-        load_part_weights(1)
+        load_part(0)
+        load_part(1)
         for r, vec in enumerate((bias, gamma, beta)):
-            nc.sync.dma_start(
+            nc.scalar.dma_start(
                 out=vec_rows[r * n_tiles : (r + 1) * n_tiles, :], in_=vec.rearrange("(j c) -> j c", c=P)
             )
-        load_part_x(1)
 
         nc.scalar.activation(out=warm_out[:], in_=warm_in[:], func=ACT.Sigmoid)
         masks.make_identity(nc, ident_f32[:])

@@ -234,10 +234,6 @@ def tile_better_transformer_s_kernel(tc, x, weights, bias, gain, norm_bias, gamm
         vec_t = psum.tile([P, P], BF16, tag="bank")
         nc.tensor.transpose(vec_t[:], vec_rows[:], ident_bf[:])
         nc.scalar.copy(out=vec_cols[:], in_=vec_t[:, 0 : 3 * n_tiles])
-        nc.gpsimd.tensor_tensor(out=beta_bias_col[:], in0=beta_col, in1=bias_col, op=ALU.mult)
-        nc.gpsimd.tensor_scalar(
-            out=rest_col[:], in0=gamma_col, scalar1=-1.0, scalar2=1.0, op0=ALU.mult, op1=ALU.add
-        )
 
         regroup_w(nc.scalar.copy, 1, D - S_COLS, D)
         regroup_w(nc.vector.tensor_copy, 1, 0, half)
@@ -245,6 +241,8 @@ def tile_better_transformer_s_kernel(tc, x, weights, bias, gain, norm_bias, gamm
         x_transposes(1, 0)
         x_transposes(1, 1)
         quantise_x(0)
+        nc.vector.tensor_tensor(out=beta_bias_col[:], in0=beta_col, in1=bias_col, op=ALU.mult)
+        nc.vector.tensor_scalar(out=rest_col[:], in0=gamma_col, scalar1=-1.0, scalar2=1.0, op0=ALU.mult, op1=ALU.add)
         normalise_x("S", 1, 0)
         normalise_x("V", 1, 1)
         multiply(0)

@@ -22,8 +22,8 @@ PAIR = 2
 WORDS = PACK // PAIR
 W_PIECES = 2
 PIECES = ((0, (0, 1)), (2, (0, 1)), (4, (0,)), (4, (1,)), (6, (0,)), (6, (1,)))
-PE_RESIDUAL = (1, 2)
-MULT_ENGINE = ("V", "V", "S", "G", "S", "G", "G", "S")
+PE_RESIDUAL = (1, 3)
+MULT_ENGINE = ("V", "V", "S", "G", "G", "G", "S", "S")
 S_COLS = 128
 
 FLOPS = 2 * BATCH * PARTS * D * D
@@ -162,24 +162,33 @@ def tile_better_transformer_s_kernel(tc, x, weights, bias, gain, norm_bias, gamm
         def product(j):
             col = slice(j, j + 1)
             act_t = work.tile([P, BATCH], F32, tag="act_t")
-            nc.vector.scalar_tensor_tensor(
-                out=act_t[:], in0=y_t[j][:], scalar=bias_col[:, col], in1=mult[j][:], op0=ALU.add, op1=ALU.mult
-            )
+            parts_of_tile = ROW_TILES if j == n_tiles - 1 else 1
+            for h in range(parts_of_tile):
+                rows = slice(h * BATCH // parts_of_tile, (h + 1) * BATCH // parts_of_tile)
+                nc.vector.scalar_tensor_tensor(
+                    out=act_t[:, rows], in0=y_t[j][:, rows], scalar=bias_col[:, col], in1=mult[j][:, rows],
+                    op0=ALU.add, op1=ALU.mult,
+                )
             p = j // COL_TILES
-            in_part = slice(j * P - p * D, (j + 1) * P - p * D)
             place = j % 2
             for n, (first, rows) in enumerate(PIECES):
                 if j - place != first:
                     continue
-                if place == 0:
+                last = place == 1
+                if not last:
                     back[n] = psum.tile([P, len(rows), 2 * P], F32, tag="bank", name="back%d" % n)
+                    if n in PE_RESIDUAL:
+                        nc.tensor.matmul(
+                            back[n][:], lhsT=ident_bf[:],
+                            rhs=x_raw[p][:, rows[0] : rows[-1] + 1, first * P - p * D : (first + 2) * P - p * D],
+                            start=True, stop=False,
+                        )
                 for r, i in enumerate(rows):
                     block = back[n][:, r, place * P : (place + 1) * P]
                     if n in PE_RESIDUAL:
-                        nc.tensor.matmul(block, lhsT=ident_bf[:], rhs=x_raw[p][:, i, in_part], start=True, stop=False)
                         nc.tensor.matmul(
                             block, lhsT=act_t[:, i * P : (i + 1) * P], rhs=ident_f32[:], is_transpose=True,
-                            start=False, stop=True,
+                            start=False, stop=last and r == len(rows) - 1,
                         )
                     else:
                         nc.tensor.transpose(block, act_t[:, i * P : (i + 1) * P], ident_f32[:])
@@ -229,32 +238,32 @@ def tile_better_transformer_s_kernel(tc, x, weights, bias, gain, norm_bias, gamm
         quantise_w(0, 0)
         quantise_w(0, 1)
         normalise_x("S", 0, 0)
-        normalise_x("S", 0, 1)
+        normalise_x("V", 0, 1)
 
         vec_t = psum.tile([P, P], BF16, tag="bank")
         nc.tensor.transpose(vec_t[:], vec_rows[:], ident_bf[:])
         nc.scalar.copy(out=vec_cols[:], in_=vec_t[:, 0 : 3 * n_tiles])
 
         regroup_w(nc.scalar.copy, 1, D - S_COLS, D)
-        regroup_w(nc.vector.tensor_copy, 1, 0, half)
-        regroup_w(nc.vector.tensor_copy, 1, half, D - S_COLS)
-        x_transposes(1, 0)
-        x_transposes(1, 1)
+        regroup_w(nc.vector.tensor_copy, 1, 0, P)
         quantise_x(0)
         nc.vector.tensor_tensor(out=beta_bias_col[:], in0=beta_col, in1=bias_col, op=ALU.mult)
         nc.vector.tensor_scalar(out=rest_col[:], in0=gamma_col, scalar1=-1.0, scalar2=1.0, op0=ALU.mult, op1=ALU.add)
+        regroup_w(nc.vector.tensor_copy, 1, P, D - S_COLS)
+        x_transposes(1, 0)
+        x_transposes(1, 1)
+        multiply(0)
         normalise_x("S", 1, 0)
         normalise_x("V", 1, 1)
-        multiply(0)
         quantise_w(1, 0)
         quantise_x(1)
-        quantise_w(1, 1)
-        multiply(1)
 
         sigmoid(0)
         sigmoid(1)
         multiplier(0)
         multiplier(1)
+        quantise_w(1, 1)
+        multiply(1)
         sigmoid(2)
         sigmoid(3)
         multiplier(3)
@@ -262,16 +271,16 @@ def tile_better_transformer_s_kernel(tc, x, weights, bias, gain, norm_bias, gamm
         product(0)
         product(1)
         sigmoid(4)
-        product(2)
-        product(3)
-        sigmoid(5)
         multiplier(4)
+        product(2)
+        sigmoid(5)
         multiplier(5)
+        product(3)
         add_residual_and_store(0)
         sigmoid(6)
+        sigmoid(7)
         multiplier(6)
         product(4)
-        sigmoid(7)
         multiplier(7)
         add_residual_and_store(1)
         product(5)

@@ -24,7 +24,7 @@ W_PIECES = 2
 PIECES = ((0, (0, 1)), (2, (0, 1)), (4, (0,)), (4, (1,)), (6, (0,)), (6, (1,)))
 PE_RESIDUAL = (1, 3)
 MULT_ENGINE = ("V", "V", "S", "G", "G", "G", "S", "S")
-S_COLS = 128
+S_COLS = (128, 256)
 
 FLOPS = 2 * BATCH * PARTS * D * D
 
@@ -229,8 +229,8 @@ def tile_better_transformer_s_kernel(tc, x, weights, bias, gain, norm_bias, gamm
         masks.make_identity(nc, ident_bf[:])
 
         regroup_w(nc.vector.tensor_copy, 0, 0, half)
-        regroup_w(nc.vector.tensor_copy, 0, half, D - S_COLS)
-        regroup_w(nc.scalar.copy, 0, D - S_COLS, D)
+        regroup_w(nc.vector.tensor_copy, 0, half, D - S_COLS[0])
+        regroup_w(nc.scalar.copy, 0, D - S_COLS[0], D)
         nc.scalar.copy(out=gain_f32[:], in_=gain_bf[:])
         nc.scalar.copy(out=shift_f32[:], in_=shift_bf[:])
         x_transposes(0, 0)
@@ -244,16 +244,16 @@ def tile_better_transformer_s_kernel(tc, x, weights, bias, gain, norm_bias, gamm
         nc.tensor.transpose(vec_t[:], vec_rows[:], ident_bf[:])
         nc.scalar.copy(out=vec_cols[:], in_=vec_t[:, 0 : 3 * n_tiles])
 
-        regroup_w(nc.scalar.copy, 1, D - S_COLS, D)
+        regroup_w(nc.scalar.copy, 1, D - S_COLS[1], D)
         regroup_w(nc.vector.tensor_copy, 1, 0, P)
         quantise_x(0)
         nc.vector.tensor_tensor(out=beta_bias_col[:], in0=beta_col, in1=bias_col, op=ALU.mult)
         nc.vector.tensor_scalar(out=rest_col[:], in0=gamma_col, scalar1=-1.0, scalar2=1.0, op0=ALU.mult, op1=ALU.add)
-        regroup_w(nc.vector.tensor_copy, 1, P, D - S_COLS)
+        regroup_w(nc.vector.tensor_copy, 1, P, D - S_COLS[1])
         x_transposes(1, 0)
         x_transposes(1, 1)
         multiply(0)
-        normalise_x("S", 1, 0)
+        normalise_x("V", 1, 0)
         normalise_x("V", 1, 1)
         quantise_w(1, 0)
         quantise_x(1)

@@ -23,7 +23,7 @@ WORDS = PACK // PAIR
 W_PIECES = 2
 PIECES = ((0, (0, 1)), (2, (0, 1)), (4, (0,)), (4, (1,)), (6, (0,)), (6, (1,)))
 PE_RESIDUAL = (1, 3)
-MULT_ENGINE = ("V", "V", "S", "G", "G", "G", "S", "S")
+MULT_ENGINE = ("V", "V", "S", "G", "G", "G", "G", "V")
 S_COLS = (128, 256)
 
 FLOPS = 2 * BATCH * PARTS * D * D
@@ -171,11 +171,10 @@ def tile_better_transformer_s_kernel(tc, x, weights, bias, gain, norm_bias, gamm
                 )
             p = j // COL_TILES
             place = j % 2
-            for n, (first, rows) in enumerate(PIECES):
-                if j - place != first:
-                    continue
-                last = place == 1
-                if not last:
+            pieces = [n for n in range(len(PIECES)) if PIECES[n][0] == j - place]
+            if place == 0:
+                for n in pieces:
+                    first, rows = PIECES[n]
                     back[n] = psum.tile([P, len(rows), 2 * P], F32, tag="bank", name="back%d" % n)
                     if n in PE_RESIDUAL:
                         nc.tensor.matmul(
@@ -183,12 +182,14 @@ def tile_better_transformer_s_kernel(tc, x, weights, bias, gain, norm_bias, gamm
                             rhs=x_raw[p][:, rows[0] : rows[-1] + 1, first * P - p * D : (first + 2) * P - p * D],
                             start=True, stop=False,
                         )
+            for n in pieces:
+                rows = PIECES[n][1]
                 for r, i in enumerate(rows):
                     block = back[n][:, r, place * P : (place + 1) * P]
                     if n in PE_RESIDUAL:
                         nc.tensor.matmul(
                             block, lhsT=act_t[:, i * P : (i + 1) * P], rhs=ident_f32[:], is_transpose=True,
-                            start=False, stop=last and r == len(rows) - 1,
+                            start=False, stop=place == 1 and r == len(rows) - 1,
                         )
                     else:
                         nc.tensor.transpose(block, act_t[:, i * P : (i + 1) * P], ident_f32[:])
@@ -278,12 +279,12 @@ def tile_better_transformer_s_kernel(tc, x, weights, bias, gain, norm_bias, gamm
         product(3)
         add_residual_and_store(0)
         sigmoid(6)
-        sigmoid(7)
         multiplier(6)
+        sigmoid(7)
         product(4)
+        product(5)
         multiplier(7)
         add_residual_and_store(1)
-        product(5)
         product(6)
         product(7)
         for n in range(2, len(PIECES)):

@@ -23,8 +23,8 @@ WORDS = PACK // PAIR
 W_PIECES = 2
 PIECES = ((0, (0, 1)), (2, (0, 1)), (4, (0,)), (4, (1,)), (6, (0,)), (6, (1,)))
 PE_RESIDUAL = (1, 3)
-MULT_ENGINE = ("V", "V", "S", "G", "G", "G", "G", "V")
-S_COLS = (128, 256)
+MULT_ENGINE = ("V", "V", "S", "G", "G", "G", "S", "V")
+S_COLS = 128
 
 FLOPS = 2 * BATCH * PARTS * D * D
 
@@ -49,8 +49,6 @@ def tile_better_transformer_s_kernel(tc, x, weights, bias, gain, norm_bias, gamm
         w_scales = [parts.tile([P, D], U8, name="w_scales%d" % p, align_bytes=64) for p in range(PARTS)]
         gain_bf = consts.tile([P, 1], BF16)
         shift_bf = consts.tile([P, 1], BF16)
-        gain_f32 = consts.tile([P, 1], F32)
-        shift_f32 = consts.tile([P, 1], F32)
         vec_rows = consts.tile([P, P], BF16)
         vec_cols = consts.tile([P, 3 * n_tiles], F32)
         bias_col = vec_cols[:, 0:n_tiles]
@@ -83,17 +81,14 @@ def tile_better_transformer_s_kernel(tc, x, weights, bias, gain, norm_bias, gamm
             for u in range(WORDS):
                 nc.tensor.transpose(x_t[p, i][:, u, :], x_words[:, i, u, :], ident_f32[:])
 
-        def normalise_x(engine, p, i):
-            grouped = x_grouped[p][:, i * P : (i + 1) * P, :].rearrange("q b (u e) -> q b u e", u=WORDS)
-            pairs = x_t[p, i][:].rearrange("q u b -> q (u b)").bitcast(BF16).rearrange(
-                "q (u b e) -> q b u e", u=WORDS, e=PAIR
+        def normalise_x(p, i):
+            nc.vector.tensor_scalar(
+                out=x_grouped[p][:, i * P : (i + 1) * P, :].rearrange("q b (u e) -> q b u e", u=WORDS),
+                in0=x_t[p, i][:].rearrange("q u b -> q (u b)").bitcast(BF16).rearrange(
+                    "q (u b e) -> q b u e", u=WORDS, e=PAIR
+                ),
+                scalar1=gain_bf[:], scalar2=shift_bf[:], op0=ALU.mult, op1=ALU.add,
             )
-            if engine == "S":
-                nc.scalar.activation(out=grouped, in_=pairs, func=ACT.Identity, bias=shift_f32[:], scale=gain_f32[:])
-            else:
-                nc.vector.tensor_scalar(
-                    out=grouped, in0=pairs, scalar1=gain_f32[:], scalar2=shift_f32[:], op0=ALU.mult, op1=ALU.add
-                )
 
         def regroup_w(copy, p, first, last):
             cols = slice(first, last)
@@ -230,40 +225,39 @@ def tile_better_transformer_s_kernel(tc, x, weights, bias, gain, norm_bias, gamm
         masks.make_identity(nc, ident_bf[:])
 
         regroup_w(nc.vector.tensor_copy, 0, 0, half)
-        regroup_w(nc.vector.tensor_copy, 0, half, D - S_COLS[0])
-        regroup_w(nc.scalar.copy, 0, D - S_COLS[0], D)
-        nc.scalar.copy(out=gain_f32[:], in_=gain_bf[:])
-        nc.scalar.copy(out=shift_f32[:], in_=shift_bf[:])
+        regroup_w(nc.vector.tensor_copy, 0, half, D - S_COLS)
+        regroup_w(nc.scalar.copy, 0, D - S_COLS, D)
         x_transposes(0, 0)
         x_transposes(0, 1)
         quantise_w(0, 0)
         quantise_w(0, 1)
-        normalise_x("S", 0, 0)
-        normalise_x("V", 0, 1)
+        normalise_x(0, 0)
+        normalise_x(0, 1)
+        regroup_w(nc.scalar.copy, 1, half, 3 * P)
 
         vec_t = psum.tile([P, P], BF16, tag="bank")
         nc.tensor.transpose(vec_t[:], vec_rows[:], ident_bf[:])
         nc.scalar.copy(out=vec_cols[:], in_=vec_t[:, 0 : 3 * n_tiles])
 
-        regroup_w(nc.scalar.copy, 1, D - S_COLS[1], D)
+        regroup_w(nc.scalar.copy, 1, 3 * P, D)
         regroup_w(nc.vector.tensor_copy, 1, 0, P)
         quantise_x(0)
         nc.vector.tensor_tensor(out=beta_bias_col[:], in0=beta_col, in1=bias_col, op=ALU.mult)
         nc.vector.tensor_scalar(out=rest_col[:], in0=gamma_col, scalar1=-1.0, scalar2=1.0, op0=ALU.mult, op1=ALU.add)
-        regroup_w(nc.vector.tensor_copy, 1, P, D - S_COLS[1])
+        regroup_w(nc.vector.tensor_copy, 1, P, half)
         x_transposes(1, 0)
         x_transposes(1, 1)
         multiply(0)
-        normalise_x("V", 1, 0)
-        normalise_x("V", 1, 1)
+        normalise_x(1, 0)
+        normalise_x(1, 1)
         quantise_w(1, 0)
         quantise_x(1)
 
         sigmoid(0)
         sigmoid(1)
         multiplier(0)
-        multiplier(1)
         quantise_w(1, 1)
+        multiplier(1)
         multiply(1)
         sigmoid(2)
         sigmoid(3)
@@ -279,8 +273,8 @@ def tile_better_transformer_s_kernel(tc, x, weights, bias, gain, norm_bias, gamm
         product(3)
         add_residual_and_store(0)
         sigmoid(6)
-        multiplier(6)
         sigmoid(7)
+        multiplier(6)
         product(4)
         product(5)
         multiplier(7)

from contextlib import ExitStack

import concourse.masks as masks
import concourse.mybir as mybir

F32 = mybir.dt.float32
BF16 = mybir.dt.bfloat16
U32 = mybir.dt.uint32
U8 = mybir.dt.uint8
FP8X4 = mybir.dt.float8_e4m3fn_x4
ACT = mybir.ActivationFunctionType
ALU = mybir.AluOpType

P = 128
PACK = 4
BATCH = 256
PARTS = 2
D = 512
ROW_TILES = BATCH // P
COL_TILES = D // P
PAIR = 2
WORDS = PACK // PAIR
W_PIECES = 2
PIECES = ((0, (0, 1)), (2, (0, 1)), (4, (0,)), (4, (1,)), (6, (0,)), (6, (1,)))
PE_RESIDUAL = (1, 3)
MULT_ENGINE = ("V", "V", "S", "G", "G", "G", "S", "V")
S_COLS = 128

FLOPS = 2 * BATCH * PARTS * D * D


def tile_better_transformer_s_kernel(tc, x, weights, bias, gain, norm_bias, gamma, beta, out):
    nc = tc.nc
    n_tiles = PARTS * COL_TILES
    with ExitStack() as ctx:
        consts = ctx.enter_context(tc.tile_pool(name="consts", bufs=1))
        parts = ctx.enter_context(tc.tile_pool(name="parts", bufs=1))
        work = ctx.enter_context(tc.tile_pool(name="work", bufs=8))
        psum = ctx.enter_context(tc.psum_pool(name="psum", bufs=8))
        ctx.enter_context(tc.manual_schedule())

        x_raw = [parts.tile([P, ROW_TILES, D], BF16, name="x_raw%d" % p) for p in range(PARTS)]
        w_raw = [parts.tile([P, PACK, D], BF16, name="w_raw%d" % p) for p in range(PARTS)]
        x_grouped = [parts.tile([P, BATCH, PACK], BF16, name="x_grouped%d" % p, align_bytes=64) for p in range(PARTS)]
        w_grouped = [parts.tile([P, D, PACK], BF16, name="w_grouped%d" % p, align_bytes=64) for p in range(PARTS)]
        x_codes = [parts.tile([P, BATCH], U32, name="x_codes%d" % p, align_bytes=64) for p in range(PARTS)]
        x_scales = [parts.tile([P, BATCH], U8, name="x_scales%d" % p, align_bytes=64) for p in range(PARTS)]
        w_codes = [parts.tile([P, D], U32, name="w_codes%d" % p, align_bytes=64) for p in range(PARTS)]
        w_scales = [parts.tile([P, D], U8, name="w_scales%d" % p, align_bytes=64) for p in range(PARTS)]
        gain_bf = consts.tile([P, 1], BF16)
        shift_bf = consts.tile([P, 1], BF16)
        vec_rows = consts.tile([P, P], BF16)
        vec_cols = consts.tile([P, 3 * n_tiles], F32)
        bias_col = vec_cols[:, 0:n_tiles]
        gamma_col = vec_cols[:, n_tiles : 2 * n_tiles]
        beta_col = vec_cols[:, 2 * n_tiles : 3 * n_tiles]
        beta_bias_col = consts.tile([P, n_tiles], F32)
        rest_col = consts.tile([P, n_tiles], F32)
        warm_in = consts.tile([P, 1], F32)
        warm_out = consts.tile([P, 1], F32)
        ident_f32 = consts.tile([P, P], F32)
        ident_bf = consts.tile([P, P], BF16)

        def load_part(p):
            nc.sync.dma_start(out=w_raw[p][:], in_=weights[p].rearrange("(q t) c -> q t c", t=PACK))
            if p < PARTS - 1:
                nc.sync.dma_start(
                    out=x_raw[p][:], in_=x[:, p * D : (p + 1) * D].rearrange("(i b) k -> b i k", b=P)
                )
            else:
                for i in range(ROW_TILES):
                    nc.sync.dma_start(out=x_raw[p][:, i, :], in_=x[i * P : (i + 1) * P, p * D : (p + 1) * D])

        x_t = {}

        def x_transposes(p, i):
            x_words = x_raw[p][:].rearrange("b i k -> b (i k)").bitcast(F32).rearrange(
                "b (i q u) -> b i u q", i=ROW_TILES, u=WORDS
            )
            x_t[p, i] = psum.tile([P, WORDS, P], F32, tag="bank", name="x_t%d_%d" % (p, i))
            for u in range(WORDS):
                nc.tensor.transpose(x_t[p, i][:, u, :], x_words[:, i, u, :], ident_f32[:])

        def normalise_x(p, i):
            nc.vector.tensor_scalar(
                out=x_grouped[p][:, i * P : (i + 1) * P, :].rearrange("q b (u e) -> q b u e", u=WORDS),
                in0=x_t[p, i][:].rearrange("q u b -> q (u b)").bitcast(BF16).rearrange(
                    "q (u b e) -> q b u e", u=WORDS, e=PAIR
                ),
                scalar1=gain_bf[:], scalar2=shift_bf[:], op0=ALU.mult, op1=ALU.add,
            )

        def regroup_w(copy, p, first, last):
            cols = slice(first, last)
            copy(
                out=w_grouped[p][:, cols, :].rearrange("q (c r) t -> q c t r", r=4),
                in_=w_raw[p][:, :, cols].rearrange("q t (c r) -> q c t r", r=4),
            )

        def quantise_w(p, h):
            cols = slice(h * D // W_PIECES, (h + 1) * D // W_PIECES)
            nc.vector.quantize_mx(
                out=w_codes[p][:, cols].bitcast(FP8X4),
                scales=w_scales[p][:, cols],
                in_=w_grouped[p][:, cols, :].rearrange("q c t -> q (c t)"),
            )

        def quantise_x(p):
            nc.vector.quantize_mx(
                out=x_codes[p][:].bitcast(FP8X4),
                scales=x_scales[p][:],
                in_=x_grouped[p][:].rearrange("q b t -> q (b t)"),
            )

        y_t = []

        def multiply(p):
            for jj in range(COL_TILES):
                cols = slice(jj * P, (jj + 1) * P)
                acc = psum.tile([P, BATCH], F32, tag="bank", name="y_t%d" % (p * COL_TILES + jj))
                nc.tensor.matmul_mx(
                    out=acc[:],
                    lhsT=w_codes[p][:, cols].bitcast(FP8X4),
                    lhsT_scale=w_scales[p][:, cols],
                    rhs=x_codes[p][:].bitcast(FP8X4),
                    rhs_scale=x_scales[p][:],
                    start=True,
                    stop=True,
                )
                y_t.append(acc)

        back = {}
        sig = {}
        mult = {}

        def sigmoid(j):
            col = slice(j, j + 1)
            sig[j] = work.tile([P, BATCH], F32, tag="sig", name="sig%d" % j)
            nc.scalar.activation(
                out=sig[j][:], in_=y_t[j][:], func=ACT.Sigmoid, bias=beta_bias_col[:, col], scale=beta_col[:, col]
            )

        def multiplier(j):
            col = slice(j, j + 1)
            mult[j] = work.tile([P, BATCH], F32, tag="mult", name="mult%d" % j)
            if MULT_ENGINE[j] == "S":
                nc.scalar.activation(
                    out=mult[j][:], in_=sig[j][:], func=ACT.Identity, bias=gamma_col[:, col], scale=rest_col[:, col]
                )
            else:
                engine = nc.vector if MULT_ENGINE[j] == "V" else nc.gpsimd
                engine.tensor_scalar(
                    out=mult[j][:], in0=sig[j][:], scalar1=rest_col[:, col], scalar2=gamma_col[:, col],
                    op0=ALU.mult, op1=ALU.add,
                )

        def product(j):
            col = slice(j, j + 1)
            act_t = work.tile([P, BATCH], F32, tag="act_t")
            parts_of_tile = ROW_TILES if j == n_tiles - 1 else 1
            for h in range(parts_of_tile):
                rows = slice(h * BATCH // parts_of_tile, (h + 1) * BATCH // parts_of_tile)
                nc.vector.scalar_tensor_tensor(
                    out=act_t[:, rows], in0=y_t[j][:, rows], scalar=bias_col[:, col], in1=mult[j][:, rows],
                    op0=ALU.add, op1=ALU.mult,
                )
            p = j // COL_TILES
            place = j % 2
            pieces = [n for n in range(len(PIECES)) if PIECES[n][0] == j - place]
            if place == 0:
                for n in pieces:
                    first, rows = PIECES[n]
                    back[n] = psum.tile([P, len(rows), 2 * P], F32, tag="bank", name="back%d" % n)
                    if n in PE_RESIDUAL:
                        nc.tensor.matmul(
                            back[n][:], lhsT=ident_bf[:],
                            rhs=x_raw[p][:, rows[0] : rows[-1] + 1, first * P - p * D : (first + 2) * P - p * D],
                            start=True, stop=False,
                        )
            for n in pieces:
                rows = PIECES[n][1]
                for r, i in enumerate(rows):
                    block = back[n][:, r, place * P : (place + 1) * P]
                    if n in PE_RESIDUAL:
                        nc.tensor.matmul(
                            block, lhsT=act_t[:, i * P : (i + 1) * P], rhs=ident_f32[:], is_transpose=True,
                            start=False, stop=place == 1 and r == len(rows) - 1,
                        )
                    else:
                        nc.tensor.transpose(block, act_t[:, i * P : (i + 1) * P], ident_f32[:])

        def add_residual_and_store(n):
            first, rows = PIECES[n]
            p = first // COL_TILES
            cols = slice(first * P, (first + 2) * P)
            in_part = slice(first * P - p * D, (first + 2) * P - p * D)
            result = parts.tile([P, len(rows), 2 * P], F32, name="result%d" % n)
            if n in PE_RESIDUAL:
                nc.scalar.copy(out=result[:], in_=back[n][:])
                queue = nc.scalar if n == PE_RESIDUAL[-1] else nc.sync
            else:
                nc.vector.tensor_tensor(
                    out=result[:], in0=back[n][:], in1=x_raw[p][:, rows[0] : rows[-1] + 1, in_part], op=ALU.add
                )
                queue = nc.sync
            queue.dma_start(
                out=out[rows[0] * P : (rows[-1] + 1) * P, cols].rearrange("(i b) c -> b i c", b=P), in_=result[:]
            )

        half = D // W_PIECES
        nc.gpsimd.memset(vec_rows[:], 0.0)
        nc.gpsimd.memset(warm_in[:], 0.0)
        with nc.allow_non_contiguous_dma(reason="one bfloat16 number to each partition"):
            nc.scalar.dma_start(out=gain_bf[:], in_=gain.partition_broadcast(P))
            nc.scalar.dma_start(out=shift_bf[:], in_=norm_bias.partition_broadcast(P))
        load_part(0)
        load_part(1)
        for r, vec in enumerate((bias, gamma, beta)):
            nc.scalar.dma_start(
                out=vec_rows[r * n_tiles : (r + 1) * n_tiles, :], in_=vec.rearrange("(j c) -> j c", c=P)
            )

        nc.scalar.activation(out=warm_out[:], in_=warm_in[:], func=ACT.Sigmoid)
        masks.make_identity(nc, ident_f32[:])
        masks.make_identity(nc, ident_bf[:])

        regroup_w(nc.vector.tensor_copy, 0, 0, half)
        regroup_w(nc.vector.tensor_copy, 0, half, D - S_COLS)
        regroup_w(nc.scalar.copy, 0, D - S_COLS, D)
        x_transposes(0, 0)
        x_transposes(0, 1)
        quantise_w(0, 0)
        quantise_w(0, 1)
        normalise_x(0, 0)
        normalise_x(0, 1)
        regroup_w(nc.scalar.copy, 1, half, 3 * P)

        vec_t = psum.tile([P, P], BF16, tag="bank")
        nc.tensor.transpose(vec_t[:], vec_rows[:], ident_bf[:])
        nc.scalar.copy(out=vec_cols[:], in_=vec_t[:, 0 : 3 * n_tiles])

        regroup_w(nc.scalar.copy, 1, 3 * P, D)
        regroup_w(nc.vector.tensor_copy, 1, 0, P)
        quantise_x(0)
        nc.vector.tensor_tensor(out=beta_bias_col[:], in0=beta_col, in1=bias_col, op=ALU.mult)
        nc.vector.tensor_scalar(out=rest_col[:], in0=gamma_col, scalar1=-1.0, scalar2=1.0, op0=ALU.mult, op1=ALU.add)
        regroup_w(nc.vector.tensor_copy, 1, P, half)
        x_transposes(1, 0)
        x_transposes(1, 1)
        multiply(0)
        normalise_x(1, 0)
        normalise_x(1, 1)
        quantise_w(1, 0)
        quantise_x(1)

        sigmoid(0)
        sigmoid(1)
        multiplier(0)
        quantise_w(1, 1)
        multiplier(1)
        multiply(1)
        sigmoid(2)
        sigmoid(3)
        multiplier(3)
        multiplier(2)
        product(0)
        product(1)
        sigmoid(4)
        multiplier(4)
        product(2)
        sigmoid(5)
        multiplier(5)
        product(3)
        add_residual_and_store(0)
        sigmoid(6)
        sigmoid(7)
        multiplier(6)
        product(4)
        product(5)
        multiplier(7)
        add_residual_and_store(1)
        product(6)
        product(7)
        for n in range(2, len(PIECES)):
            add_residual_and_store(n)
